import numpy as np
import ml_dtypes


def mxq(x, axis, fmt="e4m3"):
    dtype, down = {"e4m3": (ml_dtypes.float8_e4m3fn, 7), "e5m2": (ml_dtypes.float8_e5m2, 14)}[fmt]
    v = np.moveaxis(np.asarray(x, np.float32).astype(ml_dtypes.bfloat16).astype(np.float64), axis, -1)
    blocks = v.reshape(v.shape[:-1] + (-1, 32))
    amax = np.abs(blocks).max(-1, keepdims=True)
    byte = np.maximum(np.where(amax > 0, np.frexp(amax)[1] - 1 + 127, 0) - down, 1)
    scale = np.exp2(byte - 127.0)
    codes = (blocks / scale).astype(np.float32).astype(dtype).astype(np.float64)
    return np.moveaxis((codes * scale).reshape(v.shape), -1, axis)


WIDE = False


def mx_kscale(k):
    if not WIDE:
        return np.ones(k)
    levels = np.array([10, -10, 5, -5, 0])
    if k % 512:
        return np.exp2(np.random.permutation(np.resize(levels, k // 32))).repeat(32)
    a = np.empty((k // 512, 16))
    for p in range(k // 512):
        a[p, :8] = np.random.permutation(np.resize(levels, 8))
        for g in range(8):
            far = levels[np.abs(levels - a[p, g]) >= 10]
            a[p, g + 8] = far[np.random.randint(len(far))]
    return np.exp2(a.ravel()).repeat(32)


BF16 = ml_dtypes.bfloat16


def bf(x):
    return np.asarray(x, np.float32).astype(BF16)


def f64(x):
    return np.asarray(x).astype(np.float64)


B, N, E, L, A, H1, H2, G = 256, 8, 8, 384, 128, 1024, 1024, 8


def mish(v):
    return v * np.tanh(np.log(1.0 + np.exp(v)))


def simnorm(v):
    vg = v.reshape(v.shape[:-1] + (v.shape[-1] // G, G))
    ex = np.exp(vg - vg.max(-1, keepdims=True))
    return (ex / ex.sum(-1, keepdims=True)).reshape(v.shape)


def draw0():
    s = mx_kscale(H2)
    r = np.random.standard_normal
    return {"h2": bf(mish(r((B, E, H2))) * s),
            "logits": bf(r((B, N, E))),
            "W3": bf(r((E, H2, L)) * 2.0 / np.sqrt(H2) / s[:, None]),
            "b3": bf(0.3 * r((E, L)))}


def core(h2, logits, W3, b3):
    hq = mxq(f64(h2).transpose(1, 0, 2), 2, "e4m3")
    z = (hq @ mxq(f64(W3), 1, "e4m3")) + f64(b3)[:, None, :]
    y = simnorm(z)
    lg = f64(logits)
    ex = np.exp(lg - lg.max(-1, keepdims=True))
    comb = ex / ex.sum(-1, keepdims=True)
    return sum(comb[:, :, e, None] * y[e][:, None, :] for e in range(E))


def e4m3fn_bytes(y):
    return np.clip(np.asarray(y, np.float64), -448.0, 448.0).astype(np.float32).astype(ml_dtypes.float8_e4m3fn).view(np.uint8)


def e4m3fn_values(b):
    return np.asarray(b, np.uint8).view(ml_dtypes.float8_e4m3fn).astype(np.float64)


def setup_inputs():
    d = draw0()
    x0 = np.asarray(d['W3']).astype(np.float64)
    s = (np.max(np.abs(x0), axis=(0, 2), keepdims=True) / 448.0).astype(np.float32)
    out = {}
    for k, v in d.items():
        if k == 'W3':
            out['W3_bytes'] = e4m3fn_bytes(x0 / s.astype(np.float64))
            out['W3_scale'] = s
        else:
            out[k] = v
    return out


def reference(h2, logits, W3_bytes, W3_scale, b3):
    return core(h2, logits, e4m3fn_values(W3_bytes) * W3_scale.astype(np.float64), b3)

@@ -1,0 +1,277 @@
+from contextlib import ExitStack
+
+import concourse.mybir as mybir
+from concourse.masks import make_identity
+
+F32 = mybir.dt.float32
+BF16 = mybir.dt.bfloat16
+U32 = mybir.dt.uint32
+U8 = mybir.dt.uint8
+FP8 = mybir.dt.float8_e4m3fn
+FP8X4 = mybir.dt.float8_e4m3fn_x4
+ALU = mybir.AluOpType
+ACT = mybir.ActivationFunctionType
+AX = mybir.AxisListType
+
+B, NA, E, K, L = 256, 8, 8, 1024, 384
+P = 128
+NT = 304
+NR = L - NT
+GT = NT // 8
+FLOPS = 2 * B * E * K * L + 2 * B * NA * E * L
+
+
+def tile_softmoedynamics_pb_kernel(tc, h2, logits, W3_bytes, W3_scale, b3, out):
+    nc = tc.nc
+    with ExitStack() as ctx:
+        const = ctx.enter_context(tc.tile_pool(name="const", bufs=1))
+        loads = ctx.enter_context(tc.tile_pool(name="loads", bufs=4))
+        stage = ctx.enter_context(tc.tile_pool(name="stage", bufs=2))
+        work = ctx.enter_context(tc.tile_pool(name="work", bufs=3))
+        psA = ctx.enter_context(tc.psum_pool(name="psA", bufs=3))
+        psB = ctx.enter_context(tc.psum_pool(name="psB", bufs=3))
+        psC = ctx.enter_context(tc.psum_pool(name="psC", bufs=2))
+
+        sc = const.tile([P, 2, 4], F32, name="sc")
+        nc.sync.dma_start(
+            out=sc[:],
+            in_=W3_scale.rearrange("o k u -> (o k u)").rearrange("(g p t) -> p g t", p=P, t=4),
+        )
+        lg = const.tile([P, 2, NA * E], BF16, name="lg")
+        nc.sync.dma_start(out=lg[:], in_=logits.rearrange("(t p) n e -> p t (n e)", p=P))
+        b3pad = const.tile([P, P], BF16, name="b3pad")
+        nc.gpsimd.memset(b3pad[:], 0.0)
+        nc.sync.dma_start(out=b3pad[0 : 3 * E, :], in_=b3.rearrange("e (c p) -> (e c) p", p=P))
+        b3r = const.tile([P, E, NR], BF16, name="b3r")
+        nc.sync.dma_start(out=b3r[:], in_=b3[:, NT:L].partition_broadcast(P))
+
+        warm = const.tile([P, 2], F32, name="warm")
+        nc.vector.memset(warm[:], 0.0)
+        nc.scalar.activation(out=warm[:, 1:2], in_=warm[:, 0:1], func=ACT.Exp)
+        ident_f = const.tile([P, P], F32, name="ident_f")
+        make_identity(nc, ident_f[:])
+        ident_b = const.tile([P, P], BF16, name="ident_b")
+        make_identity(nc, ident_b[:])
+        maskb = const.tile([P, 16], F32, name="maskb")
+        nc.vector.tensor_reduce(
+            out=maskb[:], in_=ident_f[:].rearrange("p (j b) -> p b j", b=16), axis=AX.X, op=ALU.add
+        )
+
+        b3ps = psC.tile([P, P], BF16, tag="c", name="b3ps")
+        nc.tensor.transpose(b3ps[:], b3pad[:], ident_b[:])
+        b3T = const.tile([P, 3 * E], F32, name="b3T")
+        nc.vector.tensor_copy(out=b3T[:], in_=b3ps[:, 0 : 3 * E])
+
+        lg3 = lg[:].rearrange("p t (n e) -> p (t n) e", e=E)
+        lmx = const.tile([P, 16], F32, name="lmx")
+        nc.vector.tensor_reduce(out=lmx[:], in_=lg3, axis=AX.X, op=ALU.max)
+        le = const.tile([P, 16, E], F32, name="le")
+        nc.vector.tensor_tensor(
+            out=le[:], in0=lg3, in1=lmx[:].unsqueeze(2).to_broadcast([P, 16, E]), op=ALU.subtract
+        )
+        nc.scalar.activation(out=le[:], in_=le[:], func=ACT.Exp)
+        lsm = const.tile([P, 16], F32, name="lsm")
+        nc.vector.tensor_reduce(out=lsm[:], in_=le[:], axis=AX.X, op=ALU.add)
+        lrc = const.tile([P, 16], F32, name="lrc")
+        nc.vector.reciprocal(out=lrc[:], in_=lsm[:])
+        comb = const.tile([P, 16, E], F32, name="comb")
+        nc.vector.tensor_tensor(
+            out=comb[:], in0=le[:], in1=lrc[:].unsqueeze(2).to_broadcast([P, 16, E]), op=ALU.mult
+        )
+
+        bd = const.tile([P, 16, 16, NA], F32, name="bd")
+        for t in range(2):
+            gt = work.tile([P, NA * E, 16], F32, name="gt", bufs=2)
+            nc.gpsimd.tensor_tensor(
+                out=gt[:],
+                in0=comb[:, t * 8 : (t + 1) * 8, :]
+                .rearrange("p n e -> p (n e)")
+                .unsqueeze(2)
+                .to_broadcast([P, NA * E, 16]),
+                in1=maskb[:].unsqueeze(1).to_broadcast([P, NA * E, 16]),
+                op=ALU.mult,
+            )
+            for h in range(2):
+                pt = psC.tile([P, 4, P], F32, tag="c", name="pt")
+                for q in range(4):
+                    n = 4 * h + q
+                    nc.tensor.transpose(
+                        pt[:, q, :], gt[:, n * E : (n + 1) * E, :].rearrange("p e b -> p (e b)"), ident_f[:]
+                    )
+                nc.vector.tensor_copy(
+                    out=bd[:, t * 8 : (t + 1) * 8, :, 4 * h : 4 * h + 4],
+                    in_=pt[:].rearrange("p q (j b) -> p j b q", b=16),
+                )
+
+        h2v = h2.rearrange("(t p) e k -> p t e k", p=P)
+        zs = []
+        for c in range(3):
+            zs_c = const.tile([P, 16, E, 16], F32, name="zs%d" % c)
+            zs.append(zs_c)
+        zb = const.tile([P, 2, NR, E], F32, name="zb")
+        wc, ws, hc, hs = [], [], [], []
+        for e in range(E):
+            wbytes = loads.tile([P, 2, 4, L], U8, name="wbytes")
+            nc.sync.dma_start(
+                out=wbytes[:].rearrange("p g t n -> p g (t n)"),
+                in_=W3_bytes[e].rearrange("(g p t) n -> p g (t n)", p=P, t=4),
+            )
+            hraw = loads.tile([P, 2, K], BF16, name="hraw")
+            nc.sync.dma_start(out=hraw[:], in_=h2v[:, :, e, :])
+
+            wf = stage.tile([P, 2, 4, L], BF16, name="wf", bufs=3)
+            for g in range(2):
+                for t in range(4):
+                    nc.scalar.activation(
+                        out=wf[:, g, t, :],
+                        in_=wbytes[:, g, t, :].bitcast(FP8),
+                        func=ACT.Copy,
+                        scale=sc[:, g, t : t + 1],
+                    )
+            wi = stage.tile([P, 2, L, 4], BF16, name="wi", align_bytes=64)
+            nc.vector.tensor_copy(out=wi[:], in_=wf[:].rearrange("p g t n -> p g n t"))
+            wc_e = const.tile([P, 2 * L], U32, name="wc%d" % e, align_bytes=64)
+            ws_e = const.tile([P, 2 * L], U8, name="ws%d" % e, align_bytes=64)
+            wiflat = wi[:].rearrange("p g n t -> p (g n t)")
+            nc.vector.quantize_mx(
+                out=wc_e[:, 0:512].bitcast(FP8X4), scales=ws_e[:, 0:512], in_=wiflat[:, 0:2048]
+            )
+            nc.vector.quantize_mx(
+                out=wc_e[:, 512:768].bitcast(FP8X4), scales=ws_e[:, 512:768], in_=wiflat[:, 2048:3072]
+            )
+            wc.append(wc_e)
+            ws.append(ws_e)
+
+            hi = stage.tile([P, 2048], BF16, name="hi", align_bytes=64)
+            hiw = hi[:].bitcast(F32).rearrange("p (g b u) -> p g b u", g=2, u=2)
+            words = hraw[:].rearrange("p t k -> p (t k)").bitcast(F32)
+            for t in range(2):
+                xt = psA.tile([P, 4, P], F32, tag="a", name="xt")
+                for g in range(2):
+                    for u in range(2):
+                        base = t * 512 + g * 256
+                        nc.tensor.transpose(xt[:, 2 * g + u, :], words[:, base + u : base + 256 : 2], ident_f[:])
+                nc.vector.tensor_copy(
+                    out=hiw[:, :, t * P : (t + 1) * P, :], in_=xt[:].rearrange("p (g u) b -> p g b u", u=2)
+                )
+            hc_e = const.tile([P, 512], U32, name="hc%d" % e, align_bytes=64)
+            hs_e = const.tile([P, 512], U8, name="hs%d" % e, align_bytes=64)
+            nc.vector.quantize_mx(out=hc_e[:].bitcast(FP8X4), scales=hs_e[:], in_=hi[:])
+            hc.append(hc_e)
+            hs.append(hs_e)
+
+            for c in range(3):
+                zp = psB.tile([P, 256], F32, tag="b", name="zp")
+                for g in range(2):
+                    wcols = slice(g * L + c * P, g * L + (c + 1) * P)
+                    hcols = slice(g * 256, (g + 1) * 256)
+                    nc.tensor.matmul_mx(
+                        out=zp[:],
+                        lhsT=wc_e[:, wcols].bitcast(FP8X4),
+                        lhsT_scale=ws_e[:, wcols],
+                        rhs=hc_e[:, hcols].bitcast(FP8X4),
+                        rhs_scale=hs_e[:, hcols],
+                        start=(g == 0),
+                        stop=(g == 1),
+                    )
+                nc.scalar.activation(
+                    out=zs[c][:, :, e, :],
+                    in_=zp[:].rearrange("p (j b) -> p j b", b=16),
+                    func=ACT.Identity,
+                    bias=b3T[:, 3 * e + c : 3 * e + c + 1],
+                    scale=1.0,
+                )
+
+            if e % 4 == 3:
+                q4 = e - 3
+                for t in range(2):
+                    zr = psC.tile([P, 4, P], F32, tag="c", name="zr")
+                    for ei in range(4):
+                        for g in range(2):
+                            wcols = slice(g * L + 2 * P, g * L + 3 * P)
+                            hcols = slice(g * 256 + t * P, g * 256 + (t + 1) * P)
+                            nc.tensor.matmul_mx(
+                                out=zr[:, ei, :],
+                                lhsT=hc[q4 + ei][:, hcols].bitcast(FP8X4),
+                                lhsT_scale=hs[q4 + ei][:, hcols],
+                                rhs=wc[q4 + ei][:, wcols].bitcast(FP8X4),
+                                rhs_scale=ws[q4 + ei][:, wcols],
+                                start=(g == 0),
+                                stop=(g == 1),
+                            )
+                    nc.vector.tensor_tensor(
+                        out=zb[:, t, :, q4 : q4 + 4],
+                        in0=zr[:, :, P - NR : P].rearrange("p e l -> p l e"),
+                        in1=b3r[:, q4 : q4 + 4, :].rearrange("p e l -> p l e"),
+                        op=ALU.add,
+                    )
+
+        NG = 2 * NR // 8
+        zb4 = zb[:].rearrange("p t (g i) e -> p (t g) i e", i=8)
+        rmx = const.tile([P, NG, E], F32, name="rmx")
+        nc.vector.tensor_reduce(out=rmx[:], in_=zb4.rearrange("p a i e -> p a e i"), axis=AX.X, op=ALU.max)
+        ry = const.tile([P, NG, 8, E], F32, name="ry")
+        nc.vector.tensor_tensor(
+            out=ry[:], in0=zb4, in1=rmx[:].unsqueeze(2).to_broadcast([P, NG, 8, E]), op=ALU.subtract
+        )
+        nc.scalar.activation(out=ry[:], in_=ry[:], func=ACT.Exp)
+        rsm = const.tile([P, NG, E], F32, name="rsm")
+        nc.vector.tensor_reduce(out=rsm[:], in_=ry[:].rearrange("p a i e -> p a e i"), axis=AX.X, op=ALU.add)
+        rrc = const.tile([P, NG, E], F32, name="rrc")
+        nc.vector.reciprocal(out=rrc[:], in_=rsm[:])
+        nc.vector.tensor_tensor(
+            out=ry[:], in0=ry[:], in1=rrc[:].unsqueeze(2).to_broadcast([P, NG, 8, E]), op=ALU.mult
+        )
+        ryv = ry[:].rearrange("p (t g) i e -> p t (g i) e", t=2)
+
+        out_flat = out.rearrange("b n l -> (b n) l")
+        outv = out.rearrange("(t p) n l -> p t n l", p=P)
+        obs = []
+        for t in range(2):
+            ob_t = const.tile([P, NA, NR], F32, name="ob%d" % t)
+            obs.append(ob_t)
+        for j in range(16):
+            ztp = psA.tile([P, L], F32, tag="a", name="ztp")
+            for c in range(3):
+                nc.tensor.transpose(
+                    ztp[:, c * P : (c + 1) * P], zs[c][:, j, :, :].rearrange("p e b -> p (e b)"), ident_f[:]
+                )
+            z3 = ztp[:, 0:NT].rearrange("p (g i) -> p g i", i=8)
+            mx = work.tile([P, GT], F32, name="mx")
+            nc.vector.tensor_reduce(out=mx[:], in_=z3, axis=AX.X, op=ALU.max)
+            ex = work.tile([P, GT, 8], F32, name="ex")
+            nc.vector.tensor_tensor(
+                out=ex[:], in0=z3, in1=mx[:].unsqueeze(2).to_broadcast([P, GT, 8]), op=ALU.subtract
+            )
+            nc.scalar.activation(out=ex[:], in_=ex[:], func=ACT.Exp)
+            sm = work.tile([P, GT], F32, name="sm")
+            nc.vector.tensor_reduce(out=sm[:], in_=ex[:], axis=AX.X, op=ALU.add)
+            rc = work.tile([P, GT], F32, name="rc")
+            nc.vector.reciprocal(out=rc[:], in_=sm[:])
+            y = work.tile([P, GT, 8], F32, name="y")
+            nc.gpsimd.tensor_tensor(
+                out=y[:], in0=ex[:], in1=rc[:].unsqueeze(2).to_broadcast([P, GT, 8]), op=ALU.mult
+            )
+            op = psB.tile([P, NT], F32, tag="b", name="op")
+            nc.tensor.matmul(
+                op[:],
+                lhsT=bd[:, j, :, :].rearrange("p b n -> p (b n)"),
+                rhs=y[:].rearrange("p g i -> p (g i)"),
+                start=True,
+                stop=True,
+            )
+            ot = work.tile([P, NT], F32, name="ot")
+            nc.scalar.copy(out=ot[:], in_=op[:])
+            nc.sync.dma_start(out=out_flat[j * P : (j + 1) * P, 0:NT], in_=ot[:])
+
+            t, n = j // 8, j % 8
+            prod = work.tile([P, NR, E], F32, name="prod")
+            nc.gpsimd.tensor_tensor(
+                out=prod[:],
+                in0=ryv[:, t, :, :],
+                in1=comb[:, 8 * t + n, :].unsqueeze(1).to_broadcast([P, NR, E]),
+                op=ALU.mult,
+            )
+            nc.vector.tensor_reduce(out=obs[t][:, n, :], in_=prod[:], axis=AX.X, op=ALU.add)
+            if n == 7:
+                nc.sync.dma_start(out=outv[:, t, :, NT:L], in_=obs[t][:])

@@ -17,8 +17,9 @@ B, NA, E, K, L = 256, 8, 8, 1024, 384
 P = 128
 NT = 304
 NR = L - NT
-GT = NT // 8
 FLOPS = 2 * B * E * K * L + 2 * B * NA * E * L
+
+S_INTERLEAVE = ((1, 0), (1, 1), (1, 2), (1, 3), (0, 3), (0, 1))
 
 
 def tile_softmoedynamics_pb_kernel(tc, h2, logits, W3_bytes, W3_scale, b3, out):
@@ -26,7 +27,7 @@ def tile_softmoedynamics_pb_kernel(tc, h2, logits, W3_bytes, W3_scale, b3, out):
     with ExitStack() as ctx:
         const = ctx.enter_context(tc.tile_pool(name="const", bufs=1))
         loads = ctx.enter_context(tc.tile_pool(name="loads", bufs=4))
-        stage = ctx.enter_context(tc.tile_pool(name="stage", bufs=2))
+        stage = ctx.enter_context(tc.tile_pool(name="stage", bufs=3))
         work = ctx.enter_context(tc.tile_pool(name="work", bufs=3))
         psA = ctx.enter_context(tc.psum_pool(name="psA", bufs=3))
         psB = ctx.enter_context(tc.psum_pool(name="psB", bufs=3))
@@ -42,8 +43,21 @@ def tile_softmoedynamics_pb_kernel(tc, h2, logits, W3_bytes, W3_scale, b3, out):
         b3pad = const.tile([P, P], BF16, name="b3pad")
         nc.gpsimd.memset(b3pad[:], 0.0)
         nc.sync.dma_start(out=b3pad[0 : 3 * E, :], in_=b3.rearrange("e (c p) -> (e c) p", p=P))
-        b3r = const.tile([P, E, NR], BF16, name="b3r")
-        nc.sync.dma_start(out=b3r[:], in_=b3[:, NT:L].partition_broadcast(P))
+        h2v = h2.rearrange("(t p) e k -> p t e k", p=P)
+        wb, hraw = [], []
+        for e in range(E):
+            hraw_e = loads.tile([P, 2, K], BF16, name="hraw")
+            nc.sync.dma_start(out=hraw_e[:], in_=h2v[:, :, e, :])
+            hraw.append(hraw_e)
+            wb_e = const.tile([P, 2, 4, L], U8, name="wbytes%d" % e)
+            nc.sync.dma_start(
+                out=wb_e[:].rearrange("p g t n -> p g (t n)"),
+                in_=W3_bytes[e].rearrange("(g p t) n -> p g (t n)", p=P, t=4),
+            )
+            wb.append(wb_e)
+            if e == 1:
+                b3r = const.tile([P, E, NR], BF16, name="b3r")
+                nc.sync.dma_start(out=b3r[:], in_=b3[:, NT:L].partition_broadcast(P))
 
         warm = const.tile([P, 2], F32, name="warm")
         nc.vector.memset(warm[:], 0.0)
@@ -56,7 +70,6 @@ def tile_softmoedynamics_pb_kernel(tc, h2, logits, W3_bytes, W3_scale, b3, out):
         nc.vector.tensor_reduce(
             out=maskb[:], in_=ident_f[:].rearrange("p (j b) -> p b j", b=16), axis=AX.X, op=ALU.add
         )
-
         b3ps = psC.tile([P, P], BF16, tag="c", name="b3ps")
         nc.tensor.transpose(b3ps[:], b3pad[:], ident_b[:])
         b3T = const.tile([P, 3 * E], F32, name="b3T")
@@ -98,180 +111,225 @@ def tile_softmoedynamics_pb_kernel(tc, h2, logits, W3_bytes, W3_scale, b3, out):
                     nc.tensor.transpose(
                         pt[:, q, :], gt[:, n * E : (n + 1) * E, :].rearrange("p e b -> p (e b)"), ident_f[:]
                     )
-                nc.vector.tensor_copy(
+                nc.scalar.copy(
                     out=bd[:, t * 8 : (t + 1) * 8, :, 4 * h : 4 * h + 4],
                     in_=pt[:].rearrange("p q (j b) -> p j b q", b=16),
                 )
 
-        h2v = h2.rearrange("(t p) e k -> p t e k", p=P)
         zs = []
         for c in range(3):
             zs_c = const.tile([P, 16, E, 16], F32, name="zs%d" % c)
             zs.append(zs_c)
-        zb = const.tile([P, 2, NR, E], F32, name="zb")
-        wc, ws, hc, hs = [], [], [], []
-        for e in range(E):
-            wbytes = loads.tile([P, 2, 4, L], U8, name="wbytes")
-            nc.sync.dma_start(
-                out=wbytes[:].rearrange("p g t n -> p g (t n)"),
-                in_=W3_bytes[e].rearrange("(g p t) n -> p g (t n)", p=P, t=4),
-            )
-            hraw = loads.tile([P, 2, K], BF16, name="hraw")
-            nc.sync.dma_start(out=hraw[:], in_=h2v[:, :, e, :])
+        zb = const.tile([P, 2, E, NR], F32, name="zb")
+        hc, hs = [], []
+        wc, ws = {}, {}
 
-            wf = stage.tile([P, 2, 4, L], BF16, name="wf", bufs=3)
-            for g in range(2):
-                for t in range(4):
-                    nc.scalar.activation(
-                        out=wf[:, g, t, :],
-                        in_=wbytes[:, g, t, :].bitcast(FP8),
-                        func=ACT.Copy,
-                        scale=sc[:, g, t : t + 1],
-                    )
-            wi = stage.tile([P, 2, L, 4], BF16, name="wi", align_bytes=64)
-            nc.vector.tensor_copy(out=wi[:], in_=wf[:].rearrange("p g t n -> p g n t"))
-            wc_e = const.tile([P, 2 * L], U32, name="wc%d" % e, align_bytes=64)
-            ws_e = const.tile([P, 2 * L], U8, name="ws%d" % e, align_bytes=64)
-            wiflat = wi[:].rearrange("p g n t -> p (g n t)")
-            nc.vector.quantize_mx(
-                out=wc_e[:, 0:512].bitcast(FP8X4), scales=ws_e[:, 0:512], in_=wiflat[:, 0:2048]
-            )
-            nc.vector.quantize_mx(
-                out=wc_e[:, 512:768].bitcast(FP8X4), scales=ws_e[:, 512:768], in_=wiflat[:, 2048:3072]
-            )
-            wc.append(wc_e)
-            ws.append(ws_e)
-
+        def prep_h(e):
             hi = stage.tile([P, 2048], BF16, name="hi", align_bytes=64)
             hiw = hi[:].bitcast(F32).rearrange("p (g b u) -> p g b u", g=2, u=2)
-            words = hraw[:].rearrange("p t k -> p (t k)").bitcast(F32)
+            words = hraw[e][:].rearrange("p t k -> p (t k)").bitcast(F32)
             for t in range(2):
                 xt = psA.tile([P, 4, P], F32, tag="a", name="xt")
                 for g in range(2):
                     for u in range(2):
                         base = t * 512 + g * 256
                         nc.tensor.transpose(xt[:, 2 * g + u, :], words[:, base + u : base + 256 : 2], ident_f[:])
-                nc.vector.tensor_copy(
-                    out=hiw[:, :, t * P : (t + 1) * P, :], in_=xt[:].rearrange("p (g u) b -> p g b u", u=2)
-                )
+                dst = hiw[:, :, t * P : (t + 1) * P, :]
+                src = xt[:].rearrange("p (g u) b -> p g b u", u=2)
+                if t == 0:
+                    nc.scalar.copy(out=dst, in_=src)
+                else:
+                    nc.vector.tensor_copy(out=dst, in_=src)
             hc_e = const.tile([P, 512], U32, name="hc%d" % e, align_bytes=64)
             hs_e = const.tile([P, 512], U8, name="hs%d" % e, align_bytes=64)
             nc.vector.quantize_mx(out=hc_e[:].bitcast(FP8X4), scales=hs_e[:], in_=hi[:])
             hc.append(hc_e)
             hs.append(hs_e)
 
-            for c in range(3):
-                zp = psB.tile([P, 256], F32, tag="b", name="zp")
+        wfs = {}
+
+        def widen(c0, nch, ep):
+            wf = stage.tile([P, 4, 4, nch * P], BF16, name="wf%d" % nch, bufs=(2 if nch == 1 else 4))
+            for ei in range(2):
                 for g in range(2):
-                    wcols = slice(g * L + c * P, g * L + (c + 1) * P)
+                    for t in range(4):
+                        nc.scalar.activation(
+                            out=wf[:, 2 * ei + g, t, :],
+                            in_=wb[2 * ep + ei][:, g, t, c0 * P : (c0 + nch) * P].bitcast(FP8),
+                            func=ACT.Copy,
+                            scale=sc[:, g, t : t + 1],
+                        )
+            for c in range(c0, c0 + nch):
+                wfs[(c, ep)] = wf[:, :, :, (c - c0) * P : (c - c0 + 1) * P]
+
+        def pack(c, ep):
+            wi = stage.tile([P, 4, P, 4], BF16, name="wi", align_bytes=64)
+            if (c, ep) in S_INTERLEAVE:
+                nc.scalar.copy(out=wi[:], in_=wfs[(c, ep)].rearrange("p a t n -> p a n t"))
+            else:
+                nc.vector.tensor_copy(out=wi[:], in_=wfs[(c, ep)].rearrange("p a t n -> p a n t"))
+            wc_t = const.tile([P, 512], U32, name="wc%d_%d" % (c, ep), align_bytes=64)
+            ws_t = const.tile([P, 512], U8, name="ws%d_%d" % (c, ep), align_bytes=64)
+            nc.vector.quantize_mx(
+                out=wc_t[:].bitcast(FP8X4), scales=ws_t[:], in_=wi[:].rearrange("p a n t -> p (a n t)")
+            )
+            wc[(c, ep)] = wc_t
+            ws[(c, ep)] = ws_t
+
+        def mx_main(c, ep):
+            zp = psB.tile([P, 2, 256], F32, tag="b", name="zp")
+            for ei in range(2):
+                e = 2 * ep + ei
+                for g in range(2):
+                    wcols = slice((2 * ei + g) * P, (2 * ei + g + 1) * P)
                     hcols = slice(g * 256, (g + 1) * 256)
                     nc.tensor.matmul_mx(
-                        out=zp[:],
-                        lhsT=wc_e[:, wcols].bitcast(FP8X4),
-                        lhsT_scale=ws_e[:, wcols],
-                        rhs=hc_e[:, hcols].bitcast(FP8X4),
-                        rhs_scale=hs_e[:, hcols],
+                        out=zp[:, ei, :],
+                        lhsT=wc[(c, ep)][:, wcols].bitcast(FP8X4),
+                        lhsT_scale=ws[(c, ep)][:, wcols],
+                        rhs=hc[e][:, hcols].bitcast(FP8X4),
+                        rhs_scale=hs[e][:, hcols],
                         start=(g == 0),
                         stop=(g == 1),
                     )
                 nc.scalar.activation(
                     out=zs[c][:, :, e, :],
-                    in_=zp[:].rearrange("p (j b) -> p j b", b=16),
+                    in_=zp[:, ei, :].rearrange("p (j b) -> p j b", b=16),
                     func=ACT.Identity,
                     bias=b3T[:, 3 * e + c : 3 * e + c + 1],
                     scale=1.0,
                 )
 
-            if e % 4 == 3:
-                q4 = e - 3
-                for t in range(2):
-                    zr = psC.tile([P, 4, P], F32, tag="c", name="zr")
-                    for ei in range(4):
-                        for g in range(2):
-                            wcols = slice(g * L + 2 * P, g * L + 3 * P)
-                            hcols = slice(g * 256 + t * P, g * 256 + (t + 1) * P)
-                            nc.tensor.matmul_mx(
-                                out=zr[:, ei, :],
-                                lhsT=hc[q4 + ei][:, hcols].bitcast(FP8X4),
-                                lhsT_scale=hs[q4 + ei][:, hcols],
-                                rhs=wc[q4 + ei][:, wcols].bitcast(FP8X4),
-                                rhs_scale=ws[q4 + ei][:, wcols],
-                                start=(g == 0),
-                                stop=(g == 1),
-                            )
-                    nc.vector.tensor_tensor(
-                        out=zb[:, t, :, q4 : q4 + 4],
-                        in0=zr[:, :, P - NR : P].rearrange("p e l -> p l e"),
-                        in1=b3r[:, q4 : q4 + 4, :].rearrange("p e l -> p l e"),
-                        op=ALU.add,
-                    )
+        def mx_rest(q):
+            for t in range(2):
+                zr = psC.tile([P, 4, P], F32, tag="c", name="zr")
+                for k4 in range(4):
+                    e = 4 * q + k4
+                    for g in range(2):
+                        wcols = slice((2 * (e % 2) + g) * P, (2 * (e % 2) + g + 1) * P)
+                        hcols = slice(g * 256 + t * P, g * 256 + (t + 1) * P)
+                        nc.tensor.matmul_mx(
+                            out=zr[:, k4, :],
+                            lhsT=hc[e][:, hcols].bitcast(FP8X4),
+                            lhsT_scale=hs[e][:, hcols],
+                            rhs=wc[(2, e // 2)][:, wcols].bitcast(FP8X4),
+                            rhs_scale=ws[(2, e // 2)][:, wcols],
+                            start=(g == 0),
+                            stop=(g == 1),
+                        )
+                nc.vector.tensor_tensor(
+                    out=zb[:, t, 4 * q : 4 * q + 4, :],
+                    in0=zr[:, :, P - NR : P],
+                    in1=b3r[:, 4 * q : 4 * q + 4, :],
+                    op=ALU.add,
+                )
 
-        NG = 2 * NR // 8
-        zb4 = zb[:].rearrange("p t (g i) e -> p (t g) i e", i=8)
-        rmx = const.tile([P, NG, E], F32, name="rmx")
-        nc.vector.tensor_reduce(out=rmx[:], in_=zb4.rearrange("p a i e -> p a e i"), axis=AX.X, op=ALU.max)
-        ry = const.tile([P, NG, 8, E], F32, name="ry")
-        nc.vector.tensor_tensor(
-            out=ry[:], in0=zb4, in1=rmx[:].unsqueeze(2).to_broadcast([P, NG, 8, E]), op=ALU.subtract
-        )
-        nc.scalar.activation(out=ry[:], in_=ry[:], func=ACT.Exp)
-        rsm = const.tile([P, NG, E], F32, name="rsm")
-        nc.vector.tensor_reduce(out=rsm[:], in_=ry[:].rearrange("p a i e -> p a e i"), axis=AX.X, op=ALU.add)
-        rrc = const.tile([P, NG, E], F32, name="rrc")
-        nc.vector.reciprocal(out=rrc[:], in_=rsm[:])
-        nc.vector.tensor_tensor(
-            out=ry[:], in0=ry[:], in1=rrc[:].unsqueeze(2).to_broadcast([P, NG, 8, E]), op=ALU.mult
-        )
-        ryv = ry[:].rearrange("p (t g) i e -> p t (g i) e", t=2)
+        NG = 2 * E * NR // 8
+        zbg = zb[:].rearrange("p t e (g i) -> p (t e g) i", i=8)
+
+        def rest_simnorm():
+            rmx = const.tile([P, NG], F32, name="rmx")
+            nc.vector.tensor_reduce(out=rmx[:], in_=zbg, axis=AX.X, op=ALU.max)
+            nc.vector.tensor_tensor(
+                out=zbg, in0=zbg, in1=rmx[:].unsqueeze(2).to_broadcast([P, NG, 8]), op=ALU.subtract
+            )
+            nc.scalar.activation(out=zbg, in_=zbg, func=ACT.Exp)
+            rsm = const.tile([P, NG], F32, name="rsm")
+            nc.vector.tensor_reduce(out=rsm[:], in_=zbg, axis=AX.X, op=ALU.add)
+            rrc = const.tile([P, NG], F32, name="rrc")
+            nc.vector.reciprocal(out=rrc[:], in_=rsm[:])
+            nc.vector.tensor_tensor(
+                out=zbg, in0=zbg, in1=rrc[:].unsqueeze(2).to_broadcast([P, NG, 8]), op=ALU.mult
+            )
 
         out_flat = out.rearrange("b n l -> (b n) l")
+        out_tiles = out_flat.rearrange("(j p) l -> p j l", p=P)
         outv = out.rearrange("(t p) n l -> p t n l", p=P)
         obs = []
         for t in range(2):
             ob_t = const.tile([P, NA, NR], F32, name="ob%d" % t)
             obs.append(ob_t)
-        for j in range(16):
-            ztp = psA.tile([P, L], F32, tag="a", name="ztp")
-            for c in range(3):
+
+        def rest_combine(t, e):
+            for n in range(NA):
+                cs = comb[:, 8 * t + n, e : e + 1]
+                if e == 0:
+                    nc.vector.tensor_scalar(
+                        out=obs[t][:, n, :], in0=zb[:, t, e, :], scalar1=cs, scalar2=None, op0=ALU.mult
+                    )
+                else:
+                    nc.vector.scalar_tensor_tensor(
+                        out=obs[t][:, n, :], in0=zb[:, t, e, :], scalar=cs, in1=obs[t][:, n, :],
+                        op0=ALU.mult, op1=ALU.add,
+                    )
+            if e == E - 1:
+                nc.sync.dma_start(out=outv[:, t, :, NT:L], in_=obs[t][:])
+
+        def finish(c, jq):
+            w = P if c < 2 else NT - 2 * P
+            ng = w // 8
+            ztp = psA.tile([P, 4, P], F32, tag="a", name="ztp")
+            for jj in range(4):
                 nc.tensor.transpose(
-                    ztp[:, c * P : (c + 1) * P], zs[c][:, j, :, :].rearrange("p e b -> p (e b)"), ident_f[:]
+                    ztp[:, jj, :], zs[c][:, 4 * jq + jj, :, :].rearrange("p e b -> p (e b)"), ident_f[:]
                 )
-            z3 = ztp[:, 0:NT].rearrange("p (g i) -> p g i", i=8)
-            mx = work.tile([P, GT], F32, name="mx")
-            nc.vector.tensor_reduce(out=mx[:], in_=z3, axis=AX.X, op=ALU.max)
-            ex = work.tile([P, GT, 8], F32, name="ex")
+            z4 = ztp[:, :, 0:w].rearrange("p j (g i) -> p j g i", i=8)
+            mx = work.tile([P, 4, ng], F32, name="mx%d" % w)
+            nc.vector.tensor_reduce(out=mx[:], in_=z4, axis=AX.X, op=ALU.max)
+            ex = work.tile([P, 4, ng, 8], F32, name="ex%d" % w)
             nc.vector.tensor_tensor(
-                out=ex[:], in0=z3, in1=mx[:].unsqueeze(2).to_broadcast([P, GT, 8]), op=ALU.subtract
+                out=ex[:], in0=z4, in1=mx[:].unsqueeze(3).to_broadcast([P, 4, ng, 8]), op=ALU.subtract
             )
             nc.scalar.activation(out=ex[:], in_=ex[:], func=ACT.Exp)
-            sm = work.tile([P, GT], F32, name="sm")
+            sm = work.tile([P, 4, ng], F32, name="sm%d" % w)
             nc.vector.tensor_reduce(out=sm[:], in_=ex[:], axis=AX.X, op=ALU.add)
-            rc = work.tile([P, GT], F32, name="rc")
+            rc = work.tile([P, 4, ng], F32, name="rc%d" % w)
             nc.vector.reciprocal(out=rc[:], in_=sm[:])
-            y = work.tile([P, GT, 8], F32, name="y")
-            nc.gpsimd.tensor_tensor(
-                out=y[:], in0=ex[:], in1=rc[:].unsqueeze(2).to_broadcast([P, GT, 8]), op=ALU.mult
+            nc.vector.tensor_tensor(
+                out=ex[:], in0=ex[:], in1=rc[:].unsqueeze(3).to_broadcast([P, 4, ng, 8]), op=ALU.mult
             )
-            op = psB.tile([P, NT], F32, tag="b", name="op")
-            nc.tensor.matmul(
-                op[:],
-                lhsT=bd[:, j, :, :].rearrange("p b n -> p (b n)"),
-                rhs=y[:].rearrange("p g i -> p (g i)"),
-                start=True,
-                stop=True,
-            )
-            ot = work.tile([P, NT], F32, name="ot")
-            nc.scalar.copy(out=ot[:], in_=op[:])
-            nc.sync.dma_start(out=out_flat[j * P : (j + 1) * P, 0:NT], in_=ot[:])
+            op = psB.tile([P, 4, P], F32, tag="b", name="op")
+            for jj in range(4):
+                nc.tensor.matmul(
+                    op[:, jj, 0:w],
+                    lhsT=bd[:, 4 * jq + jj, :, :].rearrange("p b n -> p (b n)"),
+                    rhs=ex[:, jj, :, :].rearrange("p g i -> p (g i)"),
+                    start=True,
+                    stop=True,
+                )
+            ot = work.tile([P, 4, w], F32, name="ot%d" % w)
+            nc.scalar.copy(out=ot[:], in_=op[:, :, 0:w])
+            nc.sync.dma_start(out=out_tiles[:, 4 * jq : 4 * jq + 4, c * P : c * P + w], in_=ot[:])
 
-            t, n = j // 8, j % 8
-            prod = work.tile([P, NR, E], F32, name="prod")
-            nc.gpsimd.tensor_tensor(
-                out=prod[:],
-                in0=ryv[:, t, :, :],
-                in1=comb[:, 8 * t + n, :].unsqueeze(1).to_broadcast([P, NR, E]),
-                op=ALU.mult,
-            )
-            nc.vector.tensor_reduce(out=obs[t][:, n, :], in_=prod[:], axis=AX.X, op=ALU.add)
-            if n == 7:
-                nc.sync.dma_start(out=outv[:, t, :, NT:L], in_=obs[t][:])
+        for ep in range(4):
+            prep_h(2 * ep)
+            prep_h(2 * ep + 1)
+            widen(2, 1, ep)
+            pack(2, ep)
+            mx_main(2, ep)
+            if ep % 2 == 1:
+                mx_rest(ep // 2)
+        rest = [(t, e) for t in range(2) for e in range(E)]
+
+        def rest_units(lo, hi):
+            for te in rest[lo:hi]:
+                rest_combine(te[0], te[1])
+
+        for ep in range(4):
+            widen(0, 2, ep)
+            pack(0, ep)
+            mx_main(0, ep)
+            if ep == 0:
+                rest_simnorm()
+            finish(2, ep)
+            if ep > 0:
+                rest_units(2 * (ep - 1), 2 * ep)
+        for ep in range(4):
+            pack(1, ep)
+            mx_main(1, ep)
+            finish(0, ep)
+            rest_units(6 + ep, 7 + ep)
+        for jq in range(4):
+            finish(1, jq)
+            rest_units(10 + jq, 11 + jq)
+        rest_units(14, 16)

@@ -19,7 +19,7 @@ NT = 304
 NR = L - NT
 FLOPS = 2 * B * E * K * L + 2 * B * NA * E * L
 
-S_INTERLEAVE = ((1, 0), (1, 1), (1, 2), (1, 3), (0, 3), (0, 1))
+S_INTERLEAVE = ((1, 0), (1, 1), (1, 2), (1, 3), (0, 3))
 
 
 def tile_softmoedynamics_pb_kernel(tc, h2, logits, W3_bytes, W3_scale, b3, out):
@@ -265,7 +265,9 @@ def tile_softmoedynamics_pb_kernel(tc, h2, logits, W3_bytes, W3_scale, b3, out):
             if e == E - 1:
                 nc.sync.dma_start(out=outv[:, t, :, NT:L], in_=obs[t][:])
 
-        def finish(c, jq):
+        held = {}
+
+        def finish_a(c, jq):
             w = P if c < 2 else NT - 2 * P
             ng = w // 8
             ztp = psA.tile([P, 4, P], F32, tag="a", name="ztp")
@@ -281,6 +283,12 @@ def tile_softmoedynamics_pb_kernel(tc, h2, logits, W3_bytes, W3_scale, b3, out):
                 out=ex[:], in0=z4, in1=mx[:].unsqueeze(3).to_broadcast([P, 4, ng, 8]), op=ALU.subtract
             )
             nc.scalar.activation(out=ex[:], in_=ex[:], func=ACT.Exp)
+            held[(c, jq)] = ex
+
+        def finish_b(c, jq):
+            w = P if c < 2 else NT - 2 * P
+            ng = w // 8
+            ex = held[(c, jq)]
             sm = work.tile([P, 4, ng], F32, name="sm%d" % w)
             nc.vector.tensor_reduce(out=sm[:], in_=ex[:], axis=AX.X, op=ALU.add)
             rc = work.tile([P, 4, ng], F32, name="rc%d" % w)
@@ -321,15 +329,25 @@ def tile_softmoedynamics_pb_kernel(tc, h2, logits, W3_bytes, W3_scale, b3, out):
             mx_main(0, ep)
             if ep == 0:
                 rest_simnorm()
-            finish(2, ep)
+            finish_a(2, ep)
             if ep > 0:
+                finish_b(2, ep - 1)
                 rest_units(2 * (ep - 1), 2 * ep)
         for ep in range(4):
             pack(1, ep)
             mx_main(1, ep)
-            finish(0, ep)
+            finish_a(0, ep)
+            if ep == 0:
+                finish_b(2, 3)
+            else:
+                finish_b(0, ep - 1)
             rest_units(6 + ep, 7 + ep)
         for jq in range(4):
-            finish(1, jq)
+            finish_a(1, jq)
+            if jq == 0:
+                finish_b(0, 3)
+            else:
+                finish_b(1, jq - 1)
             rest_units(10 + jq, 11 + jq)
+        finish_b(1, 3)
         rest_units(14, 16)

@@ -15,11 +15,15 @@ AX = mybir.AxisListType
 
 B, NA, E, K, L = 256, 8, 8, 1024, 384
 P = 128
-NT = 304
-NR = L - NT
+NR = 160
+NT1 = L - NR
 FLOPS = 2 * B * E * K * L + 2 * B * NA * E * L
 
-S_INTERLEAVE = ((1, 0), (1, 1), (1, 2), (1, 3), (0, 3))
+S_PACK1 = ()
+S_PACK0 = (0, 1, 2, 3)
+UNITS = ((2, 0), (2, 1), (1, 0), (1, 1), (1, 2), (1, 3), (0, 0), (0, 1), (0, 2), (0, 3))
+G_MULT = UNITS[0:9]
+S_H2 = (0,)
 
 
 def tile_softmoedynamics_pb_kernel(tc, h2, logits, W3_bytes, W3_scale, b3, out):
@@ -28,7 +32,7 @@ def tile_softmoedynamics_pb_kernel(tc, h2, logits, W3_bytes, W3_scale, b3, out):
         const = ctx.enter_context(tc.tile_pool(name="const", bufs=1))
         loads = ctx.enter_context(tc.tile_pool(name="loads", bufs=4))
         stage = ctx.enter_context(tc.tile_pool(name="stage", bufs=3))
-        work = ctx.enter_context(tc.tile_pool(name="work", bufs=3))
+        work = ctx.enter_context(tc.tile_pool(name="work", bufs=5))
         psA = ctx.enter_context(tc.psum_pool(name="psA", bufs=3))
         psB = ctx.enter_context(tc.psum_pool(name="psB", bufs=3))
         psC = ctx.enter_context(tc.psum_pool(name="psC", bufs=2))
@@ -44,20 +48,32 @@ def tile_softmoedynamics_pb_kernel(tc, h2, logits, W3_bytes, W3_scale, b3, out):
         nc.gpsimd.memset(b3pad[:], 0.0)
         nc.sync.dma_start(out=b3pad[0 : 3 * E, :], in_=b3.rearrange("e (c p) -> (e c) p", p=P))
         h2v = h2.rearrange("(t p) e k -> p t e k", p=P)
-        wb, hraw = [], []
+        wb1, wb0, hraw = [], [], []
         for e in range(E):
             hraw_e = loads.tile([P, 2, K], BF16, name="hraw")
             nc.sync.dma_start(out=hraw_e[:], in_=h2v[:, :, e, :])
             hraw.append(hraw_e)
-            wb_e = const.tile([P, 2, 4, L], U8, name="wbytes%d" % e)
-            nc.sync.dma_start(
-                out=wb_e[:].rearrange("p g t n -> p g (t n)"),
-                in_=W3_bytes[e].rearrange("(g p t) n -> p g (t n)", p=P, t=4),
-            )
-            wb.append(wb_e)
+            if e % 2 == 0:
+                wb1_t = const.tile([P, 2, 4, 2, 256], U8, name="wbytes1_%d" % (e // 2))
+                wb1.append(wb1_t)
+            for g in range(2):
+                nc.sync.dma_start(
+                    out=wb1[e // 2][:, g, :, e % 2, :],
+                    in_=W3_bytes[e, g * 512 : (g + 1) * 512, P:L].rearrange("(p t) n -> p t n", t=4),
+                )
             if e == 1:
                 b3r = const.tile([P, E, NR], BF16, name="b3r")
-                nc.sync.dma_start(out=b3r[:], in_=b3[:, NT:L].partition_broadcast(P))
+                nc.sync.dma_start(out=b3r[:], in_=b3[:, NT1:L].partition_broadcast(P))
+
+        for e in range(E):
+            if e % 4 == 0:
+                wb0_t = const.tile([P, 2, 4, 4, P], U8, name="wbytes0_%d" % (e // 4))
+                wb0.append(wb0_t)
+            for g in range(2):
+                nc.sync.dma_start(
+                    out=wb0[e // 4][:, g, :, e % 4, :],
+                    in_=W3_bytes[e, g * 512 : (g + 1) * 512, 0:P].rearrange("(p t) n -> p t n", t=4),
+                )
 
         warm = const.tile([P, 2], F32, name="warm")
         nc.vector.memset(warm[:], 0.0)
@@ -118,9 +134,9 @@ def tile_softmoedynamics_pb_kernel(tc, h2, logits, W3_bytes, W3_scale, b3, out):
 
         zs = []
         for c in range(3):
-            zs_c = const.tile([P, 16, E, 16], F32, name="zs%d" % c)
+            zs_c = const.tile([P, 16 if c < 2 else 8, E, 16], F32, name="zs%d" % c)
             zs.append(zs_c)
-        zb = const.tile([P, 2, E, NR], F32, name="zb")
+        zb = const.tile([P, E, NR], F32, name="zb")
         hc, hs = [], []
         wc, ws = {}, {}
 
@@ -136,7 +152,7 @@ def tile_softmoedynamics_pb_kernel(tc, h2, logits, W3_bytes, W3_scale, b3, out):
                         nc.tensor.transpose(xt[:, 2 * g + u, :], words[:, base + u : base + 256 : 2], ident_f[:])
                 dst = hiw[:, :, t * P : (t + 1) * P, :]
                 src = xt[:].rearrange("p (g u) b -> p g b u", u=2)
-                if t == 0:
+                if t in S_H2:
                     nc.scalar.copy(out=dst, in_=src)
                 else:
                     nc.vector.tensor_copy(out=dst, in_=src)
@@ -146,97 +162,114 @@ def tile_softmoedynamics_pb_kernel(tc, h2, logits, W3_bytes, W3_scale, b3, out):
             hc.append(hc_e)
             hs.append(hs_e)
 
-        wfs = {}
+        def widen(wbytes):
+            wf = stage.tile([P, 2, 4, 512], BF16, name="wf", bufs=3)
+            for g in range(2):
+                for t in range(4):
+                    nc.scalar.activation(
+                        out=wf[:, g, t, :],
+                        in_=wbytes[:, g, t, :, :].rearrange("p e n -> p (e n)").bitcast(FP8),
+                        func=ACT.Copy,
+                        scale=sc[:, g, t : t + 1],
+                    )
+            return wf
 
-        def widen(c0, nch, ep):
-            wf = stage.tile([P, 4, 4, nch * P], BF16, name="wf%d" % nch, bufs=(2 if nch == 1 else 4))
-            for ei in range(2):
-                for g in range(2):
-                    for t in range(4):
-                        nc.scalar.activation(
-                            out=wf[:, 2 * ei + g, t, :],
-                            in_=wb[2 * ep + ei][:, g, t, c0 * P : (c0 + nch) * P].bitcast(FP8),
-                            func=ACT.Copy,
-                            scale=sc[:, g, t : t + 1],
-                        )
-            for c in range(c0, c0 + nch):
-                wfs[(c, ep)] = wf[:, :, :, (c - c0) * P : (c - c0 + 1) * P]
-
-        def pack(c, ep):
-            wi = stage.tile([P, 4, P, 4], BF16, name="wi", align_bytes=64)
-            if (c, ep) in S_INTERLEAVE:
-                nc.scalar.copy(out=wi[:], in_=wfs[(c, ep)].rearrange("p a t n -> p a n t"))
+        def pack(wf, half, key, on_scalar):
+            wi = stage.tile([P, 2048], BF16, name="wi", align_bytes=64)
+            dst = wi[:].rearrange("p (g n t) -> p g n t", g=2, t=4)
+            src = wf[:, :, :, 256 * half : 256 * (half + 1)].rearrange("p g t n -> p g n t")
+            if on_scalar:
+                nc.scalar.copy(out=dst, in_=src)
             else:
-                nc.vector.tensor_copy(out=wi[:], in_=wfs[(c, ep)].rearrange("p a t n -> p a n t"))
-            wc_t = const.tile([P, 512], U32, name="wc%d_%d" % (c, ep), align_bytes=64)
-            ws_t = const.tile([P, 512], U8, name="ws%d_%d" % (c, ep), align_bytes=64)
-            nc.vector.quantize_mx(
-                out=wc_t[:].bitcast(FP8X4), scales=ws_t[:], in_=wi[:].rearrange("p a n t -> p (a n t)")
-            )
-            wc[(c, ep)] = wc_t
-            ws[(c, ep)] = ws_t
+                nc.vector.tensor_copy(out=dst, in_=src)
+            wc_t = const.tile([P, 512], U32, name="wc%d_%d" % key, align_bytes=64)
+            ws_t = const.tile([P, 512], U8, name="ws%d_%d" % key, align_bytes=64)
+            nc.vector.quantize_mx(out=wc_t[:].bitcast(FP8X4), scales=ws_t[:], in_=wi[:])
+            wc[key] = wc_t
+            ws[key] = ws_t
 
-        def mx_main(c, ep):
-            zp = psB.tile([P, 2, 256], F32, tag="b", name="zp")
-            for ei in range(2):
-                e = 2 * ep + ei
+        def evac(c, e, src):
+            nc.scalar.activation(
+                out=zs[c][:, :, e, :],
+                in_=src.rearrange("p (j b) -> p j b", b=16),
+                func=ACT.Identity,
+                bias=b3T[:, 3 * e + c : 3 * e + c + 1],
+                scale=1.0,
+            )
+
+        def mx_main1(e):
+            zp = psB.tile([P, 384], F32, tag="b", name="zp1")
+            for c in (1, 2):
+                nb = 256 if c == 1 else P
+                dst = zp[:, 0:256] if c == 1 else zp[:, 256:384]
                 for g in range(2):
-                    wcols = slice((2 * ei + g) * P, (2 * ei + g + 1) * P)
-                    hcols = slice(g * 256, (g + 1) * 256)
+                    wcols = slice(g * 256 + (c - 1) * P, g * 256 + c * P)
+                    hcols = slice(g * 256, g * 256 + nb)
                     nc.tensor.matmul_mx(
-                        out=zp[:, ei, :],
-                        lhsT=wc[(c, ep)][:, wcols].bitcast(FP8X4),
-                        lhsT_scale=ws[(c, ep)][:, wcols],
+                        out=dst,
+                        lhsT=wc[(1, e)][:, wcols].bitcast(FP8X4),
+                        lhsT_scale=ws[(1, e)][:, wcols],
                         rhs=hc[e][:, hcols].bitcast(FP8X4),
                         rhs_scale=hs[e][:, hcols],
                         start=(g == 0),
                         stop=(g == 1),
                     )
-                nc.scalar.activation(
-                    out=zs[c][:, :, e, :],
-                    in_=zp[:, ei, :].rearrange("p (j b) -> p j b", b=16),
-                    func=ACT.Identity,
-                    bias=b3T[:, 3 * e + c : 3 * e + c + 1],
-                    scale=1.0,
-                )
+                evac(c, e, dst)
 
-        def mx_rest(q):
-            for t in range(2):
-                zr = psC.tile([P, 4, P], F32, tag="c", name="zr")
-                for k4 in range(4):
-                    e = 4 * q + k4
-                    for g in range(2):
-                        wcols = slice((2 * (e % 2) + g) * P, (2 * (e % 2) + g + 1) * P)
-                        hcols = slice(g * 256 + t * P, g * 256 + (t + 1) * P)
-                        nc.tensor.matmul_mx(
-                            out=zr[:, k4, :],
-                            lhsT=hc[e][:, hcols].bitcast(FP8X4),
-                            lhsT_scale=hs[e][:, hcols],
-                            rhs=wc[(2, e // 2)][:, wcols].bitcast(FP8X4),
-                            rhs_scale=ws[(2, e // 2)][:, wcols],
-                            start=(g == 0),
-                            stop=(g == 1),
-                        )
-                nc.vector.tensor_tensor(
-                    out=zb[:, t, 4 * q : 4 * q + 4, :],
-                    in0=zr[:, :, P - NR : P],
-                    in1=b3r[:, 4 * q : 4 * q + 4, :],
-                    op=ALU.add,
-                )
+        def mx_main0(ep):
+            zp = psB.tile([P, 2, 256], F32, tag="b", name="zp0")
+            for ei in range(2):
+                e = 2 * ep + ei
+                for g in range(2):
+                    wcols = slice((2 * g + ei) * P, (2 * g + ei + 1) * P)
+                    hcols = slice(g * 256, (g + 1) * 256)
+                    nc.tensor.matmul_mx(
+                        out=zp[:, ei, :],
+                        lhsT=wc[(0, ep)][:, wcols].bitcast(FP8X4),
+                        lhsT_scale=ws[(0, ep)][:, wcols],
+                        rhs=hc[e][:, hcols].bitcast(FP8X4),
+                        rhs_scale=hs[e][:, hcols],
+                        start=(g == 0),
+                        stop=(g == 1),
+                    )
+                evac(0, e, zp[:, ei, :])
 
-        NG = 2 * E * NR // 8
-        zbg = zb[:].rearrange("p t e (g i) -> p (t e g) i", i=8)
+        def mx_rest(ep):
+            zr = psC.tile([P, 2, 256], F32, tag="c", name="zr")
+            for ei in range(2):
+                e = 2 * ep + ei
+                for g in range(2):
+                    wcols = slice(g * 256, (g + 1) * 256)
+                    hcols = slice(g * 256 + P, g * 256 + 2 * P)
+                    nc.tensor.matmul_mx(
+                        out=zr[:, ei, :],
+                        lhsT=hc[e][:, hcols].bitcast(FP8X4),
+                        lhsT_scale=hs[e][:, hcols],
+                        rhs=wc[(1, e)][:, wcols].bitcast(FP8X4),
+                        rhs_scale=ws[(1, e)][:, wcols],
+                        start=(g == 0),
+                        stop=(g == 1),
+                    )
+            nc.vector.tensor_tensor(
+                out=zb[:, 2 * ep : 2 * ep + 2, :],
+                in0=zr[:, :, 256 - NR : 256],
+                in1=b3r[:, 2 * ep : 2 * ep + 2, :],
+                op=ALU.add,
+            )
 
-        def rest_simnorm():
-            rmx = const.tile([P, NG], F32, name="rmx")
+        NG = 4 * NR // 8
+
+        def rest_simnorm(q):
+            zbg = zb[:, 4 * q : 4 * q + 4, :].rearrange("p e (g i) -> p (e g) i", i=8)
+            rmx = const.tile([P, NG], F32, name="rmx%d" % q)
             nc.vector.tensor_reduce(out=rmx[:], in_=zbg, axis=AX.X, op=ALU.max)
             nc.vector.tensor_tensor(
                 out=zbg, in0=zbg, in1=rmx[:].unsqueeze(2).to_broadcast([P, NG, 8]), op=ALU.subtract
             )
             nc.scalar.activation(out=zbg, in_=zbg, func=ACT.Exp)
-            rsm = const.tile([P, NG], F32, name="rsm")
+            rsm = const.tile([P, NG], F32, name="rsm%d" % q)
             nc.vector.tensor_reduce(out=rsm[:], in_=zbg, axis=AX.X, op=ALU.add)
-            rrc = const.tile([P, NG], F32, name="rrc")
+            rrc = const.tile([P, NG], F32, name="rrc%d" % q)
             nc.vector.reciprocal(out=rrc[:], in_=rsm[:])
             nc.vector.tensor_tensor(
                 out=zbg, in0=zbg, in1=rrc[:].unsqueeze(2).to_broadcast([P, NG, 8]), op=ALU.mult
@@ -245,30 +278,26 @@ def tile_softmoedynamics_pb_kernel(tc, h2, logits, W3_bytes, W3_scale, b3, out):
         out_flat = out.rearrange("b n l -> (b n) l")
         out_tiles = out_flat.rearrange("(j p) l -> p j l", p=P)
         outv = out.rearrange("(t p) n l -> p t n l", p=P)
-        obs = []
-        for t in range(2):
-            ob_t = const.tile([P, NA, NR], F32, name="ob%d" % t)
-            obs.append(ob_t)
+        obs = const.tile([P, NA, NR], F32, name="obs")
 
-        def rest_combine(t, e):
-            for n in range(NA):
-                cs = comb[:, 8 * t + n, e : e + 1]
-                if e == 0:
-                    nc.vector.tensor_scalar(
-                        out=obs[t][:, n, :], in0=zb[:, t, e, :], scalar1=cs, scalar2=None, op0=ALU.mult
-                    )
-                else:
-                    nc.vector.scalar_tensor_tensor(
-                        out=obs[t][:, n, :], in0=zb[:, t, e, :], scalar=cs, in1=obs[t][:, n, :],
-                        op0=ALU.mult, op1=ALU.add,
-                    )
-            if e == E - 1:
-                nc.sync.dma_start(out=outv[:, t, :, NT:L], in_=obs[t][:])
+        def rest_combine(e, n):
+            cs = comb[:, 8 + n, e : e + 1]
+            if e == 0:
+                nc.vector.tensor_scalar(out=obs[:, n, :], in0=zb[:, e, :], scalar1=cs, scalar2=None, op0=ALU.mult)
+            else:
+                nc.vector.scalar_tensor_tensor(
+                    out=obs[:, n, :], in0=zb[:, e, :], scalar=cs, in1=obs[:, n, :], op0=ALU.mult, op1=ALU.add
+                )
+            if e == E - 1 and n == NA - 1:
+                nc.sync.dma_start(out=outv[:, 1, :, NT1:L], in_=obs[:])
 
         held = {}
 
+        def width(c, jq):
+            return NT1 - P if (c == 1 and jq >= 2) else P
+
         def finish_a(c, jq):
-            w = P if c < 2 else NT - 2 * P
+            w = width(c, jq)
             ng = w // 8
             ztp = psA.tile([P, 4, P], F32, tag="a", name="ztp")
             for jj in range(4):
@@ -286,14 +315,15 @@ def tile_softmoedynamics_pb_kernel(tc, h2, logits, W3_bytes, W3_scale, b3, out):
             held[(c, jq)] = ex
 
         def finish_b(c, jq):
-            w = P if c < 2 else NT - 2 * P
+            w = width(c, jq)
             ng = w // 8
             ex = held[(c, jq)]
             sm = work.tile([P, 4, ng], F32, name="sm%d" % w)
             nc.vector.tensor_reduce(out=sm[:], in_=ex[:], axis=AX.X, op=ALU.add)
             rc = work.tile([P, 4, ng], F32, name="rc%d" % w)
             nc.vector.reciprocal(out=rc[:], in_=sm[:])
-            nc.vector.tensor_tensor(
+            eng = nc.gpsimd if (c, jq) in G_MULT else nc.vector
+            eng.tensor_tensor(
                 out=ex[:], in0=ex[:], in1=rc[:].unsqueeze(3).to_broadcast([P, 4, ng, 8]), op=ALU.mult
             )
             op = psB.tile([P, 4, P], F32, tag="b", name="op")
@@ -309,45 +339,36 @@ def tile_softmoedynamics_pb_kernel(tc, h2, logits, W3_bytes, W3_scale, b3, out):
             nc.scalar.copy(out=ot[:], in_=op[:, :, 0:w])
             nc.sync.dma_start(out=out_tiles[:, 4 * jq : 4 * jq + 4, c * P : c * P + w], in_=ot[:])
 
+        rest = [(e, n) for e in range(E) for n in range(NA)]
+        done = [0]
+
+        def rest_units(k):
+            for en in rest[done[0] : done[0] + k]:
+                rest_combine(en[0], en[1])
+            done[0] = done[0] + k
+
         for ep in range(4):
             prep_h(2 * ep)
             prep_h(2 * ep + 1)
-            widen(2, 1, ep)
-            pack(2, ep)
-            mx_main(2, ep)
+            wf1 = widen(wb1[ep])
+            for e in (2 * ep, 2 * ep + 1):
+                pack(wf1, e % 2, (1, e), e in S_PACK1)
+                mx_main1(e)
+            mx_rest(ep)
             if ep % 2 == 1:
-                mx_rest(ep // 2)
-        rest = [(t, e) for t in range(2) for e in range(E)]
-
-        def rest_units(lo, hi):
-            for te in rest[lo:hi]:
-                rest_combine(te[0], te[1])
-
-        for ep in range(4):
-            widen(0, 2, ep)
-            pack(0, ep)
-            mx_main(0, ep)
-            if ep == 0:
-                rest_simnorm()
-            finish_a(2, ep)
-            if ep > 0:
-                finish_b(2, ep - 1)
-                rest_units(2 * (ep - 1), 2 * ep)
-        for ep in range(4):
-            pack(1, ep)
-            mx_main(1, ep)
-            finish_a(0, ep)
-            if ep == 0:
-                finish_b(2, 3)
-            else:
-                finish_b(0, ep - 1)
-            rest_units(6 + ep, 7 + ep)
-        for jq in range(4):
-            finish_a(1, jq)
-            if jq == 0:
-                finish_b(0, 3)
-            else:
-                finish_b(1, jq - 1)
-            rest_units(10 + jq, 11 + jq)
-        finish_b(1, 3)
-        rest_units(14, 16)
+                rest_simnorm(ep // 2)
+            if ep == 2:
+                rest_units(16)
+        fill = [6, 6, 6, 4, 4, 2, 0, 0, 0, 0]
+        for i in range(len(UNITS)):
+            if i < 4:
+                if i % 2 == 0:
+                    wf0 = widen(wb0[i // 2])
+                pack(wf0, i % 2, (0, i), i in S_PACK0)
+                mx_main0(i)
+            finish_a(UNITS[i][0], UNITS[i][1])
+            if i > 0:
+                finish_b(UNITS[i - 1][0], UNITS[i - 1][1])
+            rest_units(fill[i])
+        finish_b(UNITS[-1][0], UNITS[-1][1])
+        rest_units(len(rest) - done[0])

@@ -288,8 +288,8 @@ def tile_softmoedynamics_pb_kernel(tc, h2, logits, W3_bytes, W3_scale, b3, out):
                 nc.vector.scalar_tensor_tensor(
                     out=obs[:, n, :], in0=zb[:, e, :], scalar=cs, in1=obs[:, n, :], op0=ALU.mult, op1=ALU.add
                 )
-            if e == E - 1 and n == NA - 1:
-                nc.sync.dma_start(out=outv[:, 1, :, NT1:L], in_=obs[:])
+            if e == E - 1 and n % 2 == 1:
+                nc.sync.dma_start(out=outv[:, 1, n - 1 : n + 1, NT1:L], in_=obs[:, n - 1 : n + 1, :])
 
         held = {}
 
@@ -339,7 +339,8 @@ def tile_softmoedynamics_pb_kernel(tc, h2, logits, W3_bytes, W3_scale, b3, out):
             nc.scalar.copy(out=ot[:], in_=op[:, :, 0:w])
             nc.sync.dma_start(out=out_tiles[:, 4 * jq : 4 * jq + 4, c * P : c * P + w], in_=ot[:])
 
-        rest = [(e, n) for e in range(E) for n in range(NA)]
+        rest = [(e, n) for e in range(E - 3) for n in range(NA)]
+        rest.extend([(e, n2 + i) for n2 in range(0, NA, 2) for e in range(E - 3, E) for i in range(2)])
         done = [0]
 
         def rest_units(k):
@@ -359,7 +360,7 @@ def tile_softmoedynamics_pb_kernel(tc, h2, logits, W3_bytes, W3_scale, b3, out):
                 rest_simnorm(ep // 2)
             if ep == 2:
                 rest_units(16)
-        fill = [6, 6, 6, 4, 4, 2, 0, 0, 0, 0]
+        fill = [6, 6, 4, 4, 2, 2, 0, 0, 0, 0]
         for i in range(len(UNITS)):
             if i < 4:
                 if i % 2 == 0:

@@ -176,8 +176,8 @@ def tile_softmoedynamics_pb_kernel(tc, h2, logits, W3_bytes, W3_scale, b3, out):
 
         def pack(wf, half, key, on_scalar):
             wi = stage.tile([P, 2048], BF16, name="wi", align_bytes=64)
-            dst = wi[:].rearrange("p (g n t) -> p g n t", g=2, t=4)
-            src = wf[:, :, :, 256 * half : 256 * (half + 1)].rearrange("p g t n -> p g n t")
+            dst = wi[:].rearrange("p (g c i t) -> p g c t i", g=2, i=4, t=4)
+            src = wf[:, :, :, 256 * half : 256 * (half + 1)].rearrange("p g t (c i) -> p g c t i", i=4)
             if on_scalar:
                 nc.scalar.copy(out=dst, in_=src)
             else:

@@ -140,6 +140,8 @@ def tile_softmoedynamics_pb_kernel(tc, h2, logits, W3_bytes, W3_scale, b3, out):
         hc, hs = [], []
         wc, ws = {}, {}
 
+        his = {}
+
         def prep_h(e):
             hi = stage.tile([P, 2048], BF16, name="hi", align_bytes=64)
             hiw = hi[:].bitcast(F32).rearrange("p (g b u) -> p g b u", g=2, u=2)
@@ -156,9 +158,12 @@ def tile_softmoedynamics_pb_kernel(tc, h2, logits, W3_bytes, W3_scale, b3, out):
                     nc.scalar.copy(out=dst, in_=src)
                 else:
                     nc.vector.tensor_copy(out=dst, in_=src)
+            his[e] = hi
+
+        def quant_h(e):
             hc_e = const.tile([P, 512], U32, name="hc%d" % e, align_bytes=64)
             hs_e = const.tile([P, 512], U8, name="hs%d" % e, align_bytes=64)
-            nc.vector.quantize_mx(out=hc_e[:].bitcast(FP8X4), scales=hs_e[:], in_=hi[:])
+            nc.vector.quantize_mx(out=hc_e[:].bitcast(FP8X4), scales=hs_e[:], in_=his[e][:])
             hc.append(hc_e)
             hs.append(hs_e)
 
@@ -182,6 +187,9 @@ def tile_softmoedynamics_pb_kernel(tc, h2, logits, W3_bytes, W3_scale, b3, out):
                 nc.scalar.copy(out=dst, in_=src)
             else:
                 nc.vector.tensor_copy(out=dst, in_=src)
+            return wi
+
+        def quant(wi, key):
             wc_t = const.tile([P, 512], U32, name="wc%d_%d" % key, align_bytes=64)
             ws_t = const.tile([P, 512], U8, name="ws%d_%d" % key, align_bytes=64)
             nc.vector.quantize_mx(out=wc_t[:].bitcast(FP8X4), scales=ws_t[:], in_=wi[:])
@@ -234,8 +242,11 @@ def tile_softmoedynamics_pb_kernel(tc, h2, logits, W3_bytes, W3_scale, b3, out):
                     )
                 evac(0, e, zp[:, ei, :])
 
+        zrs = {}
+
         def mx_rest(ep):
             zr = psC.tile([P, 2, 256], F32, tag="c", name="zr")
+            zrs[ep] = zr
             for ei in range(2):
                 e = 2 * ep + ei
                 for g in range(2):
@@ -250,23 +261,31 @@ def tile_softmoedynamics_pb_kernel(tc, h2, logits, W3_bytes, W3_scale, b3, out):
                         start=(g == 0),
                         stop=(g == 1),
                     )
+
+        def rest_add(ep):
             nc.vector.tensor_tensor(
                 out=zb[:, 2 * ep : 2 * ep + 2, :],
-                in0=zr[:, :, 256 - NR : 256],
+                in0=zrs[ep][:, :, 256 - NR : 256],
                 in1=b3r[:, 2 * ep : 2 * ep + 2, :],
                 op=ALU.add,
             )
 
-        NG = 4 * NR // 8
+        NG = 2 * NR // 8
 
-        def rest_simnorm(q):
-            zbg = zb[:, 4 * q : 4 * q + 4, :].rearrange("p e (g i) -> p (e g) i", i=8)
+        def zb_groups(q):
+            return zb[:, 2 * q : 2 * q + 2, :].rearrange("p e (g i) -> p (e g) i", i=8)
+
+        def rest_simnorm_a(q):
+            zbg = zb_groups(q)
             rmx = const.tile([P, NG], F32, name="rmx%d" % q)
             nc.vector.tensor_reduce(out=rmx[:], in_=zbg, axis=AX.X, op=ALU.max)
             nc.vector.tensor_tensor(
                 out=zbg, in0=zbg, in1=rmx[:].unsqueeze(2).to_broadcast([P, NG, 8]), op=ALU.subtract
             )
             nc.scalar.activation(out=zbg, in_=zbg, func=ACT.Exp)
+
+        def rest_simnorm_b(q):
+            zbg = zb_groups(q)
             rsm = const.tile([P, NG], F32, name="rsm%d" % q)
             nc.vector.tensor_reduce(out=rsm[:], in_=zbg, axis=AX.X, op=ALU.add)
             rrc = const.tile([P, NG], F32, name="rrc%d" % q)
@@ -348,28 +367,50 @@ def tile_softmoedynamics_pb_kernel(tc, h2, logits, W3_bytes, W3_scale, b3, out):
                 rest_combine(en[0], en[1])
             done[0] = done[0] + k
 
+        wfq = []
+        prep_h(0)
+        prep_h(1)
+        wfq.append(widen(wb1[0]))
+        quant_h(0)
+        quant_h(1)
         for ep in range(4):
-            prep_h(2 * ep)
-            prep_h(2 * ep + 1)
-            wf1 = widen(wb1[ep])
-            for e in (2 * ep, 2 * ep + 1):
-                pack(wf1, e % 2, (1, e), e in S_PACK1)
-                mx_main1(e)
+            if ep < 3:
+                prep_h(2 * ep + 2)
+                prep_h(2 * ep + 3)
+                wfq.append(widen(wb1[ep + 1]))
+            else:
+                wfq.append(widen(wb0[0]))
+            wia = pack(wfq[ep], 0, (1, 2 * ep), 2 * ep in S_PACK1)
+            wib = pack(wfq[ep], 1, (1, 2 * ep + 1), 2 * ep + 1 in S_PACK1)
+            if ep < 3:
+                quant_h(2 * ep + 2)
+                quant_h(2 * ep + 3)
+            quant(wia, (1, 2 * ep))
+            quant(wib, (1, 2 * ep + 1))
+            mx_main1(2 * ep)
+            mx_main1(2 * ep + 1)
             mx_rest(ep)
-            if ep % 2 == 1:
-                rest_simnorm(ep // 2)
-            if ep == 2:
-                rest_units(16)
-        fill = [6, 6, 4, 4, 2, 2, 0, 0, 0, 0]
+            if ep > 0:
+                rest_add(ep - 1)
+                rest_simnorm_a(ep - 1)
+            if ep > 1:
+                rest_simnorm_b(ep - 2)
+                rest_units(8 if ep == 2 else 24)
+        rest_add(3)
+        rest_simnorm_a(3)
+        rest_simnorm_b(2)
+        fill = [4, 4, 0, 0, 0, 0, 0, 0, 0, 0]
         for i in range(len(UNITS)):
             if i < 4:
-                if i % 2 == 0:
-                    wf0 = widen(wb0[i // 2])
-                pack(wf0, i % 2, (0, i), i in S_PACK0)
+                if i == 1:
+                    wfq.append(widen(wb0[1]))
+                quant(pack(wfq[4 + i // 2], i % 2, (0, i), i in S_PACK0), (0, i))
                 mx_main0(i)
             finish_a(UNITS[i][0], UNITS[i][1])
             if i > 0:
                 finish_b(UNITS[i - 1][0], UNITS[i - 1][1])
+            if i == 1:
+                rest_simnorm_b(3)
             rest_units(fill[i])
         finish_b(UNITS[-1][0], UNITS[-1][1])
         rest_units(len(rest) - done[0])

@@ -23,7 +23,7 @@ S_PACK1 = ()
 S_PACK0 = (0, 1, 2, 3)
 UNITS = ((2, 0), (2, 1), (1, 0), (1, 1), (1, 2), (1, 3), (0, 0), (0, 1), (0, 2), (0, 3))
 G_MULT = UNITS[0:9]
-S_H2 = (0,)
+V_H2 = (0, 1)
 
 
 def tile_softmoedynamics_pb_kernel(tc, h2, logits, W3_bytes, W3_scale, b3, out):
@@ -154,10 +154,10 @@ def tile_softmoedynamics_pb_kernel(tc, h2, logits, W3_bytes, W3_scale, b3, out):
                         nc.tensor.transpose(xt[:, 2 * g + u, :], words[:, base + u : base + 256 : 2], ident_f[:])
                 dst = hiw[:, :, t * P : (t + 1) * P, :]
                 src = xt[:].rearrange("p (g u) b -> p g b u", u=2)
-                if t in S_H2:
-                    nc.scalar.copy(out=dst, in_=src)
-                else:
+                if t == 1 and e in V_H2:
                     nc.vector.tensor_copy(out=dst, in_=src)
+                else:
+                    nc.scalar.copy(out=dst, in_=src)
             his[e] = hi
 
         def quant_h(e):
@@ -167,16 +167,17 @@ def tile_softmoedynamics_pb_kernel(tc, h2, logits, W3_bytes, W3_scale, b3, out):
             hc.append(hc_e)
             hs.append(hs_e)
 
-        def widen(wbytes):
+        def widen(wbytes, v_slots=()):
             wf = stage.tile([P, 2, 4, 512], BF16, name="wf", bufs=3)
             for g in range(2):
                 for t in range(4):
-                    nc.scalar.activation(
-                        out=wf[:, g, t, :],
-                        in_=wbytes[:, g, t, :, :].rearrange("p e n -> p (e n)").bitcast(FP8),
-                        func=ACT.Copy,
-                        scale=sc[:, g, t : t + 1],
-                    )
+                    codes = wbytes[:, g, t, :, :].rearrange("p e n -> p (e n)").bitcast(FP8)
+                    if t in v_slots:
+                        nc.vector.tensor_scalar(
+                            out=wf[:, g, t, :], in0=codes, scalar1=sc[:, g, t : t + 1], scalar2=None, op0=ALU.mult
+                        )
+                    else:
+                        nc.scalar.activation(out=wf[:, g, t, :], in_=codes, func=ACT.Copy, scale=sc[:, g, t : t + 1])
             return wf
 
         def pack(wf, half, key, on_scalar):
@@ -377,7 +378,7 @@ def tile_softmoedynamics_pb_kernel(tc, h2, logits, W3_bytes, W3_scale, b3, out):
             if ep < 3:
                 prep_h(2 * ep + 2)
                 prep_h(2 * ep + 3)
-                wfq.append(widen(wb1[ep + 1]))
+                wfq.append(widen(wb1[ep + 1], (3,)))
             else:
                 wfq.append(widen(wb0[0]))
             wia = pack(wfq[ep], 0, (1, 2 * ep), 2 * ep in S_PACK1)
@@ -403,7 +404,7 @@ def tile_softmoedynamics_pb_kernel(tc, h2, logits, W3_bytes, W3_scale, b3, out):
         for i in range(len(UNITS)):
             if i < 4:
                 if i == 1:
-                    wfq.append(widen(wb0[1]))
+                    wfq.append(widen(wb0[1], (2, 3)))
                 quant(pack(wfq[4 + i // 2], i % 2, (0, i), i in S_PACK0), (0, i))
                 mx_main0(i)
             finish_a(UNITS[i][0], UNITS[i][1])

@@ -109,9 +109,11 @@ def tile_softmoedynamics_pb_kernel(tc, h2, logits, W3_bytes, W3_scale, b3, out):
         )
 
         bd = const.tile([P, 16, 16, NA], F32, name="bd")
-        for t in range(2):
+        gts = []
+
+        def bd_products(t):
             gt = work.tile([P, NA * E, 16], F32, name="gt", bufs=2)
-            nc.gpsimd.tensor_tensor(
+            nc.vector.tensor_tensor(
                 out=gt[:],
                 in0=comb[:, t * 8 : (t + 1) * 8, :]
                 .rearrange("p n e -> p (n e)")
@@ -120,12 +122,15 @@ def tile_softmoedynamics_pb_kernel(tc, h2, logits, W3_bytes, W3_scale, b3, out):
                 in1=maskb[:].unsqueeze(1).to_broadcast([P, NA * E, 16]),
                 op=ALU.mult,
             )
+            gts.append(gt)
+
+        def bd_turn(t):
             for h in range(2):
                 pt = psC.tile([P, 4, P], F32, tag="c", name="pt")
                 for q in range(4):
                     n = 4 * h + q
                     nc.tensor.transpose(
-                        pt[:, q, :], gt[:, n * E : (n + 1) * E, :].rearrange("p e b -> p (e b)"), ident_f[:]
+                        pt[:, q, :], gts[t][:, n * E : (n + 1) * E, :].rearrange("p e b -> p (e b)"), ident_f[:]
                     )
                 nc.scalar.copy(
                     out=bd[:, t * 8 : (t + 1) * 8, :, 4 * h : 4 * h + 4],
@@ -374,6 +379,8 @@ def tile_softmoedynamics_pb_kernel(tc, h2, logits, W3_bytes, W3_scale, b3, out):
         wfq.append(widen(wb1[0]))
         quant_h(0)
         quant_h(1)
+        bd_products(0)
+        bd_products(1)
         for ep in range(4):
             if ep < 3:
                 prep_h(2 * ep + 2)
@@ -397,6 +404,7 @@ def tile_softmoedynamics_pb_kernel(tc, h2, logits, W3_bytes, W3_scale, b3, out):
             if ep > 1:
                 rest_simnorm_b(ep - 2)
                 rest_units(8 if ep == 2 else 24)
+                bd_turn(ep - 2)
         rest_add(3)
         rest_simnorm_a(3)
         rest_simnorm_b(2)

@@ -211,6 +211,8 @@ def tile_softmoedynamics_pb_kernel(tc, h2, logits, W3_bytes, W3_scale, b3, out):
                 scale=1.0,
             )
 
+        zp1s = {}
+
         def mx_main1(e):
             zp = psB.tile([P, 384], F32, tag="b", name="zp1")
             for c in (1, 2):
@@ -228,7 +230,11 @@ def tile_softmoedynamics_pb_kernel(tc, h2, logits, W3_bytes, W3_scale, b3, out):
                         start=(g == 0),
                         stop=(g == 1),
                     )
-                evac(c, e, dst)
+            zp1s[e] = zp
+
+        def evac_main1(e):
+            evac(1, e, zp1s[e][:, 0:256])
+            evac(2, e, zp1s[e][:, 256:384])
 
         def mx_main0(ep):
             zp = psB.tile([P, 2, 256], F32, tag="b", name="zp0")
@@ -351,7 +357,11 @@ def tile_softmoedynamics_pb_kernel(tc, h2, logits, W3_bytes, W3_scale, b3, out):
             eng.tensor_tensor(
                 out=ex[:], in0=ex[:], in1=rc[:].unsqueeze(3).to_broadcast([P, 4, ng, 8]), op=ALU.mult
             )
-            op = psB.tile([P, 4, P], F32, tag="b", name="op")
+
+        def finish_c(c, jq):
+            w = width(c, jq)
+            ex = held[(c, jq)]
+            op = psC.tile([P, 4, P], F32, tag="c", name="op")
             for jj in range(4):
                 nc.tensor.matmul(
                     op[:, jj, 0:w],
@@ -388,6 +398,9 @@ def tile_softmoedynamics_pb_kernel(tc, h2, logits, W3_bytes, W3_scale, b3, out):
                 wfq.append(widen(wb1[ep + 1], (3,)))
             else:
                 wfq.append(widen(wb0[0]))
+            if ep > 0:
+                evac_main1(2 * ep - 2)
+                evac_main1(2 * ep - 1)
             wia = pack(wfq[ep], 0, (1, 2 * ep), 2 * ep in S_PACK1)
             wib = pack(wfq[ep], 1, (1, 2 * ep + 1), 2 * ep + 1 in S_PACK1)
             if ep < 3:
@@ -405,6 +418,8 @@ def tile_softmoedynamics_pb_kernel(tc, h2, logits, W3_bytes, W3_scale, b3, out):
                 rest_simnorm_b(ep - 2)
                 rest_units(8 if ep == 2 else 24)
                 bd_turn(ep - 2)
+        evac_main1(6)
+        evac_main1(7)
         rest_add(3)
         rest_simnorm_a(3)
         rest_simnorm_b(2)
@@ -418,8 +433,12 @@ def tile_softmoedynamics_pb_kernel(tc, h2, logits, W3_bytes, W3_scale, b3, out):
             finish_a(UNITS[i][0], UNITS[i][1])
             if i > 0:
                 finish_b(UNITS[i - 1][0], UNITS[i - 1][1])
+            if i > 1:
+                finish_c(UNITS[i - 2][0], UNITS[i - 2][1])
             if i == 1:
                 rest_simnorm_b(3)
             rest_units(fill[i])
+        finish_c(UNITS[-2][0], UNITS[-2][1])
         finish_b(UNITS[-1][0], UNITS[-1][1])
+        finish_c(UNITS[-1][0], UNITS[-1][1])
         rest_units(len(rest) - done[0])

@@ -33,8 +33,8 @@ def tile_softmoedynamics_pb_kernel(tc, h2, logits, W3_bytes, W3_scale, b3, out):
         loads = ctx.enter_context(tc.tile_pool(name="loads", bufs=4))
         stage = ctx.enter_context(tc.tile_pool(name="stage", bufs=3))
         work = ctx.enter_context(tc.tile_pool(name="work", bufs=5))
-        psA = ctx.enter_context(tc.psum_pool(name="psA", bufs=3))
-        psB = ctx.enter_context(tc.psum_pool(name="psB", bufs=3))
+        psA = ctx.enter_context(tc.psum_pool(name="psA", bufs=4))
+        psB = ctx.enter_context(tc.psum_pool(name="psB", bufs=2))
         psC = ctx.enter_context(tc.psum_pool(name="psC", bufs=2))
 
         sc = const.tile([P, 2, 4], F32, name="sc")
@@ -147,18 +147,24 @@ def tile_softmoedynamics_pb_kernel(tc, h2, logits, W3_bytes, W3_scale, b3, out):
 
         his = {}
 
-        def prep_h(e):
-            hi = stage.tile([P, 2048], BF16, name="hi", align_bytes=64)
-            hiw = hi[:].bitcast(F32).rearrange("p (g b u) -> p g b u", g=2, u=2)
+        xts = {}
+
+        def turn_h(e):
             words = hraw[e][:].rearrange("p t k -> p (t k)").bitcast(F32)
             for t in range(2):
                 xt = psA.tile([P, 4, P], F32, tag="a", name="xt")
+                xts[(e, t)] = xt
                 for g in range(2):
                     for u in range(2):
                         base = t * 512 + g * 256
                         nc.tensor.transpose(xt[:, 2 * g + u, :], words[:, base + u : base + 256 : 2], ident_f[:])
+
+        def empty_h(e):
+            hi = stage.tile([P, 2048], BF16, name="hi", align_bytes=64)
+            hiw = hi[:].bitcast(F32).rearrange("p (g b u) -> p g b u", g=2, u=2)
+            for t in range(2):
                 dst = hiw[:, :, t * P : (t + 1) * P, :]
-                src = xt[:].rearrange("p (g u) b -> p g b u", u=2)
+                src = xts[(e, t)][:].rearrange("p (g u) b -> p g b u", u=2)
                 if t == 1 and e in V_H2:
                     nc.vector.tensor_copy(out=dst, in_=src)
                 else:
@@ -384,8 +390,10 @@ def tile_softmoedynamics_pb_kernel(tc, h2, logits, W3_bytes, W3_scale, b3, out):
             done[0] = done[0] + k
 
         wfq = []
-        prep_h(0)
-        prep_h(1)
+        turn_h(0)
+        empty_h(0)
+        turn_h(1)
+        empty_h(1)
         wfq.append(widen(wb1[0]))
         quant_h(0)
         quant_h(1)
@@ -393,8 +401,8 @@ def tile_softmoedynamics_pb_kernel(tc, h2, logits, W3_bytes, W3_scale, b3, out):
         bd_products(1)
         for ep in range(4):
             if ep < 3:
-                prep_h(2 * ep + 2)
-                prep_h(2 * ep + 3)
+                turn_h(2 * ep + 2)
+                turn_h(2 * ep + 3)
                 wfq.append(widen(wb1[ep + 1], (3,)))
             else:
                 wfq.append(widen(wb0[0]))
@@ -403,11 +411,11 @@ def tile_softmoedynamics_pb_kernel(tc, h2, logits, W3_bytes, W3_scale, b3, out):
                 evac_main1(2 * ep - 1)
             wia = pack(wfq[ep], 0, (1, 2 * ep), 2 * ep in S_PACK1)
             wib = pack(wfq[ep], 1, (1, 2 * ep + 1), 2 * ep + 1 in S_PACK1)
-            if ep < 3:
-                quant_h(2 * ep + 2)
-                quant_h(2 * ep + 3)
             quant(wia, (1, 2 * ep))
             quant(wib, (1, 2 * ep + 1))
+            if ep < 3:
+                empty_h(2 * ep + 2)
+                empty_h(2 * ep + 3)
             mx_main1(2 * ep)
             mx_main1(2 * ep + 1)
             mx_rest(ep)
@@ -418,6 +426,9 @@ def tile_softmoedynamics_pb_kernel(tc, h2, logits, W3_bytes, W3_scale, b3, out):
                 rest_simnorm_b(ep - 2)
                 rest_units(8 if ep == 2 else 24)
                 bd_turn(ep - 2)
+            if ep < 3:
+                quant_h(2 * ep + 2)
+                quant_h(2 * ep + 3)
         evac_main1(6)
         evac_main1(7)
         rest_add(3)

@@ -442,13 +442,13 @@ def tile_softmoedynamics_pb_kernel(tc, h2, logits, W3_bytes, W3_scale, b3, out):
                 quant(pack(wfq[4 + i // 2], i % 2, (0, i), i in S_PACK0), (0, i))
                 mx_main0(i)
             finish_a(UNITS[i][0], UNITS[i][1])
+            if i == 1:
+                rest_simnorm_b(3)
+            rest_units(fill[i])
             if i > 0:
                 finish_b(UNITS[i - 1][0], UNITS[i - 1][1])
             if i > 1:
                 finish_c(UNITS[i - 2][0], UNITS[i - 2][1])
-            if i == 1:
-                rest_simnorm_b(3)
-            rest_units(fill[i])
         finish_c(UNITS[-2][0], UNITS[-2][1])
         finish_b(UNITS[-1][0], UNITS[-1][1])
         finish_c(UNITS[-1][0], UNITS[-1][1])

@@ -394,7 +394,7 @@ def tile_softmoedynamics_pb_kernel(tc, h2, logits, W3_bytes, W3_scale, b3, out):
         empty_h(0)
         turn_h(1)
         empty_h(1)
-        wfq.append(widen(wb1[0]))
+        wfq.append(widen(wb1[0], (2, 3)))
         quant_h(0)
         quant_h(1)
         bd_products(0)

@@ -42,28 +42,43 @@ def tile_softmoedynamics_pb_kernel(tc, h2, logits, W3_bytes, W3_scale, b3, out):
             out=sc[:],
             in_=W3_scale.rearrange("o k u -> (o k u)").rearrange("(g p t) -> p g t", p=P, t=4),
         )
+        h2v = h2.rearrange("(t p) e k -> p t e k", p=P)
+        wb1, wb0, hraw = [], [], []
+
+        def load_h(e):
+            hraw_e = loads.tile([P, 2, K], BF16, name="hraw")
+            nc.sync.dma_start(out=hraw_e[:], in_=h2v[:, :, e, :])
+            hraw.append(hraw_e)
+
+        def load_w1(ep):
+            wb1_t = const.tile([P, 2, 4, 2, 256], U8, name="wbytes1_%d" % ep)
+            wb1.append(wb1_t)
+            for g in range(2):
+                for ei in range(2):
+                    nc.sync.dma_start(
+                        out=wb1_t[:, g, :, ei, :],
+                        in_=W3_bytes[2 * ep + ei, g * 512 : (g + 1) * 512, P:L].rearrange("(p t) n -> p t n", t=4),
+                    )
+
         lg = const.tile([P, 2, NA * E], BF16, name="lg")
         nc.sync.dma_start(out=lg[:], in_=logits.rearrange("(t p) n e -> p t (n e)", p=P))
         b3pad = const.tile([P, P], BF16, name="b3pad")
         nc.gpsimd.memset(b3pad[:], 0.0)
         nc.sync.dma_start(out=b3pad[0 : 3 * E, :], in_=b3.rearrange("e (c p) -> (e c) p", p=P))
-        h2v = h2.rearrange("(t p) e k -> p t e k", p=P)
-        wb1, wb0, hraw = [], [], []
-        for e in range(E):
-            hraw_e = loads.tile([P, 2, K], BF16, name="hraw")
-            nc.sync.dma_start(out=hraw_e[:], in_=h2v[:, :, e, :])
-            hraw.append(hraw_e)
-            if e % 2 == 0:
-                wb1_t = const.tile([P, 2, 4, 2, 256], U8, name="wbytes1_%d" % (e // 2))
-                wb1.append(wb1_t)
-            for g in range(2):
-                nc.sync.dma_start(
-                    out=wb1[e // 2][:, g, :, e % 2, :],
-                    in_=W3_bytes[e, g * 512 : (g + 1) * 512, P:L].rearrange("(p t) n -> p t n", t=4),
-                )
-            if e == 1:
-                b3r = const.tile([P, E, NR], BF16, name="b3r")
-                nc.sync.dma_start(out=b3r[:], in_=b3[:, NT1:L].partition_broadcast(P))
+        load_h(0)
+        load_w1(0)
+        load_h(1)
+        load_w1(1)
+        load_h(2)
+        load_h(3)
+        load_w1(2)
+        b3r = const.tile([P, E, NR], BF16, name="b3r")
+        nc.sync.dma_start(out=b3r[:], in_=b3[:, NT1:L].partition_broadcast(P))
+        load_h(4)
+        load_h(5)
+        load_w1(3)
+        load_h(6)
+        load_h(7)
 
         for e in range(E):
             if e % 4 == 0:

@@ -23,7 +23,7 @@ S_PACK1 = ()
 S_PACK0 = (0, 1, 2, 3)
 UNITS = ((2, 0), (2, 1), (1, 0), (1, 1), (1, 2), (1, 3), (0, 0), (0, 1), (0, 2), (0, 3))
 G_MULT = UNITS[0:9]
-V_H2 = (0, 1)
+V_H2 = (0,)
 
 
 def tile_softmoedynamics_pb_kernel(tc, h2, logits, W3_bytes, W3_scale, b3, out):
@@ -175,7 +175,7 @@ def tile_softmoedynamics_pb_kernel(tc, h2, logits, W3_bytes, W3_scale, b3, out):
                         nc.tensor.transpose(xt[:, 2 * g + u, :], words[:, base + u : base + 256 : 2], ident_f[:])
 
         def empty_h(e):
-            hi = stage.tile([P, 2048], BF16, name="hi", align_bytes=64)
+            hi = stage.tile([P, 2048], BF16, name="hi", align_bytes=64, bufs=4)
             hiw = hi[:].bitcast(F32).rearrange("p (g b u) -> p g b u", g=2, u=2)
             for t in range(2):
                 dst = hiw[:, :, t * P : (t + 1) * P, :]
@@ -405,15 +405,13 @@ def tile_softmoedynamics_pb_kernel(tc, h2, logits, W3_bytes, W3_scale, b3, out):
             done[0] = done[0] + k
 
         wfq = []
+        bd_products(0)
+        bd_products(1)
         turn_h(0)
         empty_h(0)
         turn_h(1)
-        empty_h(1)
         wfq.append(widen(wb1[0], (2, 3)))
-        quant_h(0)
-        quant_h(1)
-        bd_products(0)
-        bd_products(1)
+        empty_h(1)
         for ep in range(4):
             if ep < 3:
                 turn_h(2 * ep + 2)
@@ -428,6 +426,8 @@ def tile_softmoedynamics_pb_kernel(tc, h2, logits, W3_bytes, W3_scale, b3, out):
             wib = pack(wfq[ep], 1, (1, 2 * ep + 1), 2 * ep + 1 in S_PACK1)
             quant(wia, (1, 2 * ep))
             quant(wib, (1, 2 * ep + 1))
+            quant_h(2 * ep)
+            quant_h(2 * ep + 1)
             if ep < 3:
                 empty_h(2 * ep + 2)
                 empty_h(2 * ep + 3)
@@ -441,9 +441,6 @@ def tile_softmoedynamics_pb_kernel(tc, h2, logits, W3_bytes, W3_scale, b3, out):
                 rest_simnorm_b(ep - 2)
                 rest_units(8 if ep == 2 else 24)
                 bd_turn(ep - 2)
-            if ep < 3:
-                quant_h(2 * ep + 2)
-                quant_h(2 * ep + 3)
         evac_main1(6)
         evac_main1(7)
         rest_add(3)

@@ -73,22 +73,31 @@ def tile_softmoedynamics_pb_kernel(tc, h2, logits, W3_bytes, W3_scale, b3, out):
         load_h(3)
         load_w1(2)
         b3r = const.tile([P, E, NR], BF16, name="b3r")
-        nc.sync.dma_start(out=b3r[:], in_=b3[:, NT1:L].partition_broadcast(P))
+
+        def load_b3r(q):
+            nc.sync.dma_start(out=b3r[:, 2 * q : 2 * q + 2, :], in_=b3[2 * q : 2 * q + 2, NT1:L].partition_broadcast(P))
+
+        def load_w0(eq):
+            wb0_t = const.tile([P, 2, 4, 4, P], U8, name="wbytes0_%d" % eq)
+            wb0.append(wb0_t)
+            for g in range(2):
+                for ei in range(4):
+                    nc.sync.dma_start(
+                        out=wb0_t[:, g, :, ei, :],
+                        in_=W3_bytes[4 * eq + ei, g * 512 : (g + 1) * 512, 0:P].rearrange("(p t) n -> p t n", t=4),
+                    )
+
+        load_b3r(0)
         load_h(4)
         load_h(5)
         load_w1(3)
         load_h(6)
         load_h(7)
-
-        for e in range(E):
-            if e % 4 == 0:
-                wb0_t = const.tile([P, 2, 4, 4, P], U8, name="wbytes0_%d" % (e // 4))
-                wb0.append(wb0_t)
-            for g in range(2):
-                nc.sync.dma_start(
-                    out=wb0[e // 4][:, g, :, e % 4, :],
-                    in_=W3_bytes[e, g * 512 : (g + 1) * 512, 0:P].rearrange("(p t) n -> p t n", t=4),
-                )
+        load_b3r(1)
+        load_w0(0)
+        load_b3r(2)
+        load_w0(1)
+        load_b3r(3)
 
         warm = const.tile([P, 2], F32, name="warm")
         nc.vector.memset(warm[:], 0.0)

@@ -37,6 +37,8 @@ def tile_softmoedynamics_pb_kernel(tc, h2, logits, W3_bytes, W3_scale, b3, out):
         psB = ctx.enter_context(tc.psum_pool(name="psB", bufs=2))
         psC = ctx.enter_context(tc.psum_pool(name="psC", bufs=2))
 
+        lg = const.tile([P, 2, NA * E], BF16, name="lg")
+        nc.sync.dma_start(out=lg[:], in_=logits.rearrange("(t p) n e -> p t (n e)", p=P))
         sc = const.tile([P, 2, 4], F32, name="sc")
         nc.sync.dma_start(
             out=sc[:],
@@ -60,13 +62,11 @@ def tile_softmoedynamics_pb_kernel(tc, h2, logits, W3_bytes, W3_scale, b3, out):
                         in_=W3_bytes[2 * ep + ei, g * 512 : (g + 1) * 512, P:L].rearrange("(p t) n -> p t n", t=4),
                     )
 
-        lg = const.tile([P, 2, NA * E], BF16, name="lg")
-        nc.sync.dma_start(out=lg[:], in_=logits.rearrange("(t p) n e -> p t (n e)", p=P))
         b3pad = const.tile([P, P], BF16, name="b3pad")
         nc.gpsimd.memset(b3pad[:], 0.0)
-        nc.sync.dma_start(out=b3pad[0 : 3 * E, :], in_=b3.rearrange("e (c p) -> (e c) p", p=P))
-        load_h(0)
         load_w1(0)
+        load_h(0)
+        nc.sync.dma_start(out=b3pad[0 : 3 * E, :], in_=b3.rearrange("e (c p) -> (e c) p", p=P))
         load_h(1)
         load_w1(1)
         load_h(2)
@@ -416,10 +416,10 @@ def tile_softmoedynamics_pb_kernel(tc, h2, logits, W3_bytes, W3_scale, b3, out):
         wfq = []
         bd_products(0)
         bd_products(1)
+        wfq.append(widen(wb1[0], (2, 3)))
         turn_h(0)
         empty_h(0)
         turn_h(1)
-        wfq.append(widen(wb1[0], (2, 3)))
         empty_h(1)
         for ep in range(4):
             if ep < 3:

@@ -106,10 +106,6 @@ def tile_softmoedynamics_pb_kernel(tc, h2, logits, W3_bytes, W3_scale, b3, out):
         make_identity(nc, ident_f[:])
         ident_b = const.tile([P, P], BF16, name="ident_b")
         make_identity(nc, ident_b[:])
-        maskb = const.tile([P, 16], F32, name="maskb")
-        nc.vector.tensor_reduce(
-            out=maskb[:], in_=ident_f[:].rearrange("p (j b) -> p b j", b=16), axis=AX.X, op=ALU.add
-        )
         b3ps = psC.tile([P, P], BF16, tag="c", name="b3ps")
         nc.tensor.transpose(b3ps[:], b3pad[:], ident_b[:])
         b3T = const.tile([P, 3 * E], F32, name="b3T")
@@ -127,39 +123,21 @@ def tile_softmoedynamics_pb_kernel(tc, h2, logits, W3_bytes, W3_scale, b3, out):
         nc.vector.tensor_reduce(out=lsm[:], in_=le[:], axis=AX.X, op=ALU.add)
         lrc = const.tile([P, 16], F32, name="lrc")
         nc.vector.reciprocal(out=lrc[:], in_=lsm[:])
-        comb = const.tile([P, 16, E], F32, name="comb")
+        comb = const.tile([P, 2, E, NA], F32, name="comb")
         nc.vector.tensor_tensor(
-            out=comb[:], in0=le[:], in1=lrc[:].unsqueeze(2).to_broadcast([P, 16, E]), op=ALU.mult
+            out=comb[:].rearrange("p t e n -> p t n e"),
+            in0=le[:].rearrange("p (t n) e -> p t n e", t=2),
+            in1=lrc[:].rearrange("p (t n) -> p t n", t=2).unsqueeze(3).to_broadcast([P, 2, NA, E]),
+            op=ALU.mult,
         )
 
         bd = const.tile([P, 16, 16, NA], F32, name="bd")
-        gts = []
-
-        def bd_products(t):
-            gt = work.tile([P, NA * E, 16], F32, name="gt", bufs=2)
-            nc.vector.tensor_tensor(
-                out=gt[:],
-                in0=comb[:, t * 8 : (t + 1) * 8, :]
-                .rearrange("p n e -> p (n e)")
-                .unsqueeze(2)
-                .to_broadcast([P, NA * E, 16]),
-                in1=maskb[:].unsqueeze(1).to_broadcast([P, NA * E, 16]),
-                op=ALU.mult,
-            )
-            gts.append(gt)
-
-        def bd_turn(t):
-            for h in range(2):
-                pt = psC.tile([P, 4, P], F32, tag="c", name="pt")
-                for q in range(4):
-                    n = 4 * h + q
-                    nc.tensor.transpose(
-                        pt[:, q, :], gts[t][:, n * E : (n + 1) * E, :].rearrange("p e b -> p (e b)"), ident_f[:]
-                    )
-                nc.scalar.copy(
-                    out=bd[:, t * 8 : (t + 1) * 8, :, 4 * h : 4 * h + 4],
-                    in_=pt[:].rearrange("p q (j b) -> p j b q", b=16),
-                )
+        nc.gpsimd.memset(bd[:], 0.0)
+        park = out.rearrange("b n l -> (b n l)")[0 : B * E * NA]
+        nc.sync.dma_start(out=park.rearrange("(t p x) -> p t x", p=P, x=E * NA), in_=comb[:].rearrange("p t e n -> p t (e n)"))
+        back = park.rearrange("(j b e n) -> b e j n", b=16, e=E, n=NA)
+        for bl in range(16):
+            nc.sync.dma_start(out=bd[bl : P : 16, :, bl, :], in_=back[bl])
 
         zs = []
         for c in range(3):
@@ -342,7 +320,7 @@ def tile_softmoedynamics_pb_kernel(tc, h2, logits, W3_bytes, W3_scale, b3, out):
         obs = const.tile([P, NA, NR], F32, name="obs")
 
         def rest_combine(e, n):
-            cs = comb[:, 8 + n, e : e + 1]
+            cs = comb[:, 1, e, n : n + 1]
             if e == 0:
                 nc.vector.tensor_scalar(out=obs[:, n, :], in0=zb[:, e, :], scalar1=cs, scalar2=None, op0=ALU.mult)
             else:
@@ -414,8 +392,6 @@ def tile_softmoedynamics_pb_kernel(tc, h2, logits, W3_bytes, W3_scale, b3, out):
             done[0] = done[0] + k
 
         wfq = []
-        bd_products(0)
-        bd_products(1)
         wfq.append(widen(wb1[0], (2, 3)))
         turn_h(0)
         empty_h(0)
@@ -425,7 +401,7 @@ def tile_softmoedynamics_pb_kernel(tc, h2, logits, W3_bytes, W3_scale, b3, out):
             if ep < 3:
                 turn_h(2 * ep + 2)
                 turn_h(2 * ep + 3)
-                wfq.append(widen(wb1[ep + 1], (3,)))
+                wfq.append(widen(wb1[ep + 1]))
             else:
                 wfq.append(widen(wb0[0]))
             if ep > 0:
@@ -449,7 +425,6 @@ def tile_softmoedynamics_pb_kernel(tc, h2, logits, W3_bytes, W3_scale, b3, out):
             if ep > 1:
                 rest_simnorm_b(ep - 2)
                 rest_units(8 if ep == 2 else 24)
-                bd_turn(ep - 2)
         evac_main1(6)
         evac_main1(7)
         rest_add(3)

@@ -66,9 +66,9 @@ def tile_softmoedynamics_pb_kernel(tc, h2, logits, W3_bytes, W3_scale, b3, out):
         nc.gpsimd.memset(b3pad[:], 0.0)
         load_w1(0)
         load_h(0)
-        nc.sync.dma_start(out=b3pad[0 : 3 * E, :], in_=b3.rearrange("e (c p) -> (e c) p", p=P))
-        load_h(1)
         load_w1(1)
+        load_h(1)
+        nc.sync.dma_start(out=b3pad[0 : 3 * E, :], in_=b3.rearrange("e (c p) -> (e c) p", p=P))
         load_h(2)
         load_h(3)
         load_w1(2)

@@ -22,7 +22,7 @@ FLOPS = 2 * B * E * K * L + 2 * B * NA * E * L
 S_PACK1 = ()
 S_PACK0 = (0, 1, 2, 3)
 UNITS = ((2, 0), (2, 1), (1, 0), (1, 1), (1, 2), (1, 3), (0, 0), (0, 1), (0, 2), (0, 3))
-G_MULT = UNITS[0:9]
+G_MULT = UNITS[0:8]
 V_H2 = (0,)
 
 

@@ -195,8 +195,8 @@ def tile_softmoedynamics_pb_kernel(tc, h2, logits, W3_bytes, W3_scale, b3, out):
 
         def pack(wf, half, key, on_scalar):
             wi = stage.tile([P, 2048], BF16, name="wi", align_bytes=64)
-            dst = wi[:].rearrange("p (g c i t) -> p g c t i", g=2, i=4, t=4)
-            src = wf[:, :, :, 256 * half : 256 * (half + 1)].rearrange("p g t (c i) -> p g c t i", i=4)
+            dst = wi[:].rearrange("p (g c i t) -> p g c t i", g=2, i=8, t=4)
+            src = wf[:, :, :, 256 * half : 256 * (half + 1)].rearrange("p g t (c i) -> p g c t i", i=8)
             if on_scalar:
                 nc.scalar.copy(out=dst, in_=src)
             else:

@@ -401,7 +401,7 @@ def tile_softmoedynamics_pb_kernel(tc, h2, logits, W3_bytes, W3_scale, b3, out):
             if ep < 3:
                 turn_h(2 * ep + 2)
                 turn_h(2 * ep + 3)
-                wfq.append(widen(wb1[ep + 1]))
+                wfq.append(widen(wb1[ep + 1], (3,) if ep < 2 else ()))
             else:
                 wfq.append(widen(wb0[0]))
             if ep > 0:

@@ -262,6 +262,40 @@ def tile_softmoedynamics_pb_kernel(tc, h2, logits, W3_bytes, W3_scale, b3, out):
                     )
                 evac(0, e, zp[:, ei, :])
 
+        def last_pair_by_pass(wf, half, ep):
+            wi = stage.tile([P, 2048], BF16, name="wi", align_bytes=64)
+            wc_t = const.tile([P, 512], U32, name="wc0_%d" % ep, align_bytes=64)
+            ws_t = const.tile([P, 512], U8, name="ws0_%d" % ep, align_bytes=64)
+            zpe = []
+            for ei in range(2):
+                zp = psB.tile([P, 256], F32, tag="b", name="zp0e")
+                zpe.append(zp)
+            for g in range(2):
+                nc.scalar.copy(
+                    out=wi[:, g * 1024 : (g + 1) * 1024].rearrange("p (c i t) -> p c t i", i=8, t=4),
+                    in_=wf[:, g, :, 256 * half : 256 * (half + 1)].rearrange("p t (c i) -> p c t i", i=8),
+                )
+                nc.vector.quantize_mx(
+                    out=wc_t[:, g * 256 : (g + 1) * 256].bitcast(FP8X4),
+                    scales=ws_t[:, g * 256 : (g + 1) * 256],
+                    in_=wi[:, g * 1024 : (g + 1) * 1024],
+                )
+                for ei in range(2):
+                    e = 2 * ep + ei
+                    wcols = slice((2 * g + ei) * P, (2 * g + ei + 1) * P)
+                    hcols = slice(g * 256, (g + 1) * 256)
+                    nc.tensor.matmul_mx(
+                        out=zpe[ei][:],
+                        lhsT=wc_t[:, wcols].bitcast(FP8X4),
+                        lhsT_scale=ws_t[:, wcols],
+                        rhs=hc[e][:, hcols].bitcast(FP8X4),
+                        rhs_scale=hs[e][:, hcols],
+                        start=(g == 0),
+                        stop=(g == 1),
+                    )
+            for ei in range(2):
+                evac(0, 2 * ep + ei, zpe[ei][:])
+
         zrs = {}
 
         def mx_rest(ep):
@@ -435,8 +469,11 @@ def tile_softmoedynamics_pb_kernel(tc, h2, logits, W3_bytes, W3_scale, b3, out):
             if i < 4:
                 if i == 1:
                     wfq.append(widen(wb0[1], (2, 3)))
-                quant(pack(wfq[4 + i // 2], i % 2, (0, i), i in S_PACK0), (0, i))
-                mx_main0(i)
+                if i < 3:
+                    quant(pack(wfq[4 + i // 2], i % 2, (0, i), i in S_PACK0), (0, i))
+                    mx_main0(i)
+                else:
+                    last_pair_by_pass(wfq[4 + i // 2], i % 2, i)
             finish_a(UNITS[i][0], UNITS[i][1])
             if i == 1:
                 rest_simnorm_b(3)

@@ -262,6 +262,23 @@ def tile_softmoedynamics_pb_kernel(tc, h2, logits, W3_bytes, W3_scale, b3, out):
                     )
                 evac(0, e, zp[:, ei, :])
 
+        def pack_quant_by_pass(wf, half, key):
+            wi = stage.tile([P, 2048], BF16, name="wi", align_bytes=64)
+            wc_t = const.tile([P, 512], U32, name="wc%d_%d" % key, align_bytes=64)
+            ws_t = const.tile([P, 512], U8, name="ws%d_%d" % key, align_bytes=64)
+            for g in range(2):
+                nc.scalar.copy(
+                    out=wi[:, g * 1024 : (g + 1) * 1024].rearrange("p (c i t) -> p c t i", i=8, t=4),
+                    in_=wf[:, g, :, 256 * half : 256 * (half + 1)].rearrange("p t (c i) -> p c t i", i=8),
+                )
+                nc.vector.quantize_mx(
+                    out=wc_t[:, g * 256 : (g + 1) * 256].bitcast(FP8X4),
+                    scales=ws_t[:, g * 256 : (g + 1) * 256],
+                    in_=wi[:, g * 1024 : (g + 1) * 1024],
+                )
+            wc[key] = wc_t
+            ws[key] = ws_t
+
         def last_pair_by_pass(wf, half, ep):
             wi = stage.tile([P, 2048], BF16, name="wi", align_bytes=64)
             wc_t = const.tile([P, 512], U32, name="wc0_%d" % ep, align_bytes=64)
@@ -469,8 +486,11 @@ def tile_softmoedynamics_pb_kernel(tc, h2, logits, W3_bytes, W3_scale, b3, out):
             if i < 4:
                 if i == 1:
                     wfq.append(widen(wb0[1], (2, 3)))
-                if i < 3:
+                if i < 2:
                     quant(pack(wfq[4 + i // 2], i % 2, (0, i), i in S_PACK0), (0, i))
+                    mx_main0(i)
+                elif i == 2:
+                    pack_quant_by_pass(wfq[4 + i // 2], i % 2, (0, i))
                     mx_main0(i)
                 else:
                     last_pair_by_pass(wfq[4 + i // 2], i % 2, i)

@@ -21,7 +21,9 @@ FLOPS = 2 * B * E * K * L + 2 * B * NA * E * L
 
 S_PACK1 = ()
 S_PACK0 = (0, 1, 2, 3)
-UNITS = ((2, 0), (2, 1), (1, 0), (1, 1), (1, 2), (1, 3), (0, 0), (0, 1), (0, 2), (0, 3))
+UNITS = (
+    (2, 0, 4), (2, 4, 4), (1, 0, 4), (1, 4, 4), (1, 8, 4), (1, 12, 4), (0, 0, 4), (0, 4, 4), (0, 8, 4), (0, 12, 2), (0, 14, 2)
+)
 G_MULT = UNITS[0:8]
 V_H2 = (0,)
 
@@ -383,55 +385,55 @@ def tile_softmoedynamics_pb_kernel(tc, h2, logits, W3_bytes, W3_scale, b3, out):
 
         held = {}
 
-        def width(c, jq):
-            return NT1 - P if (c == 1 and jq >= 2) else P
+        def width(c, j0):
+            return NT1 - P if (c == 1 and j0 >= 8) else P
 
-        def finish_a(c, jq):
-            w = width(c, jq)
+        def finish_a(c, j0, nt):
+            w = width(c, j0)
             ng = w // 8
             ztp = psA.tile([P, 4, P], F32, tag="a", name="ztp")
-            for jj in range(4):
+            for jj in range(nt):
                 nc.tensor.transpose(
-                    ztp[:, jj, :], zs[c][:, 4 * jq + jj, :, :].rearrange("p e b -> p (e b)"), ident_f[:]
+                    ztp[:, jj, :], zs[c][:, j0 + jj, :, :].rearrange("p e b -> p (e b)"), ident_f[:]
                 )
-            z4 = ztp[:, :, 0:w].rearrange("p j (g i) -> p j g i", i=8)
-            mx = work.tile([P, 4, ng], F32, name="mx%d" % w)
+            z4 = ztp[:, 0:nt, 0:w].rearrange("p j (g i) -> p j g i", i=8)
+            mx = work.tile([P, nt, ng], F32, name="mx%d" % w)
             nc.vector.tensor_reduce(out=mx[:], in_=z4, axis=AX.X, op=ALU.max)
-            ex = work.tile([P, 4, ng, 8], F32, name="ex%d" % w)
+            ex = work.tile([P, nt, ng, 8], F32, name="ex%d" % w)
             nc.vector.tensor_tensor(
-                out=ex[:], in0=z4, in1=mx[:].unsqueeze(3).to_broadcast([P, 4, ng, 8]), op=ALU.subtract
+                out=ex[:], in0=z4, in1=mx[:].unsqueeze(3).to_broadcast([P, nt, ng, 8]), op=ALU.subtract
             )
             nc.scalar.activation(out=ex[:], in_=ex[:], func=ACT.Exp)
-            held[(c, jq)] = ex
+            held[(c, j0)] = ex
 
-        def finish_b(c, jq):
-            w = width(c, jq)
+        def finish_b(c, j0, nt):
+            w = width(c, j0)
             ng = w // 8
-            ex = held[(c, jq)]
-            sm = work.tile([P, 4, ng], F32, name="sm%d" % w)
+            ex = held[(c, j0)]
+            sm = work.tile([P, nt, ng], F32, name="sm%d" % w)
             nc.vector.tensor_reduce(out=sm[:], in_=ex[:], axis=AX.X, op=ALU.add)
-            rc = work.tile([P, 4, ng], F32, name="rc%d" % w)
+            rc = work.tile([P, nt, ng], F32, name="rc%d" % w)
             nc.vector.reciprocal(out=rc[:], in_=sm[:])
-            eng = nc.gpsimd if (c, jq) in G_MULT else nc.vector
+            eng = nc.gpsimd if (c, j0, nt) in G_MULT else nc.vector
             eng.tensor_tensor(
-                out=ex[:], in0=ex[:], in1=rc[:].unsqueeze(3).to_broadcast([P, 4, ng, 8]), op=ALU.mult
+                out=ex[:], in0=ex[:], in1=rc[:].unsqueeze(3).to_broadcast([P, nt, ng, 8]), op=ALU.mult
             )
 
-        def finish_c(c, jq):
-            w = width(c, jq)
-            ex = held[(c, jq)]
+        def finish_c(c, j0, nt):
+            w = width(c, j0)
+            ex = held[(c, j0)]
             op = psC.tile([P, 4, P], F32, tag="c", name="op")
-            for jj in range(4):
+            for jj in range(nt):
                 nc.tensor.matmul(
                     op[:, jj, 0:w],
-                    lhsT=bd[:, 4 * jq + jj, :, :].rearrange("p b n -> p (b n)"),
+                    lhsT=bd[:, j0 + jj, :, :].rearrange("p b n -> p (b n)"),
                     rhs=ex[:, jj, :, :].rearrange("p g i -> p (g i)"),
                     start=True,
                     stop=True,
                 )
-            ot = work.tile([P, 4, w], F32, name="ot%d" % w)
-            nc.scalar.copy(out=ot[:], in_=op[:, :, 0:w])
-            nc.sync.dma_start(out=out_tiles[:, 4 * jq : 4 * jq + 4, c * P : c * P + w], in_=ot[:])
+            ot = work.tile([P, nt, w], F32, name="ot%d" % w)
+            nc.scalar.copy(out=ot[:], in_=op[:, 0:nt, 0:w])
+            nc.sync.dma_start(out=out_tiles[:, j0 : j0 + nt, c * P : c * P + w], in_=ot[:])
 
         rest = [(e, n) for e in range(E - 3) for n in range(NA)]
         rest.extend([(e, n2 + i) for n2 in range(0, NA, 2) for e in range(E - 3, E) for i in range(2)])
@@ -481,7 +483,7 @@ def tile_softmoedynamics_pb_kernel(tc, h2, logits, W3_bytes, W3_scale, b3, out):
         rest_add(3)
         rest_simnorm_a(3)
         rest_simnorm_b(2)
-        fill = [4, 4, 0, 0, 0, 0, 0, 0, 0, 0]
+        fill = [4, 4, 0, 0, 0, 0, 0, 0, 0, 0, 0]
         for i in range(len(UNITS)):
             if i < 4:
                 if i == 1:
@@ -494,15 +496,15 @@ def tile_softmoedynamics_pb_kernel(tc, h2, logits, W3_bytes, W3_scale, b3, out):
                     mx_main0(i)
                 else:
                     last_pair_by_pass(wfq[4 + i // 2], i % 2, i)
-            finish_a(UNITS[i][0], UNITS[i][1])
+            finish_a(UNITS[i][0], UNITS[i][1], UNITS[i][2])
             if i == 1:
                 rest_simnorm_b(3)
             rest_units(fill[i])
             if i > 0:
-                finish_b(UNITS[i - 1][0], UNITS[i - 1][1])
+                finish_b(UNITS[i - 1][0], UNITS[i - 1][1], UNITS[i - 1][2])
             if i > 1:
-                finish_c(UNITS[i - 2][0], UNITS[i - 2][1])
-        finish_c(UNITS[-2][0], UNITS[-2][1])
-        finish_b(UNITS[-1][0], UNITS[-1][1])
-        finish_c(UNITS[-1][0], UNITS[-1][1])
+                finish_c(UNITS[i - 2][0], UNITS[i - 2][1], UNITS[i - 2][2])
+        finish_c(UNITS[-2][0], UNITS[-2][1], UNITS[-2][2])
+        finish_b(UNITS[-1][0], UNITS[-1][1], UNITS[-1][2])
+        finish_c(UNITS[-1][0], UNITS[-1][1], UNITS[-1][2])
         rest_units(len(rest) - done[0])

@@ -19,7 +19,6 @@ NR = 160
 NT1 = L - NR
 FLOPS = 2 * B * E * K * L + 2 * B * NA * E * L
 
-S_PACK1 = ()
 S_PACK0 = (0, 1, 2, 3)
 UNITS = (
     (2, 0, 4), (2, 4, 4), (1, 0, 4), (1, 4, 4), (1, 8, 4), (1, 12, 4), (0, 0, 4), (0, 4, 4), (0, 8, 4), (0, 12, 2), (0, 14, 2)
@@ -164,8 +163,11 @@ def tile_softmoedynamics_pb_kernel(tc, h2, logits, W3_bytes, W3_scale, b3, out):
                         nc.tensor.transpose(xt[:, 2 * g + u, :], words[:, base + u : base + 256 : 2], ident_f[:])
 
         def empty_h(e):
-            hi = stage.tile([P, 2048], BF16, name="hi", align_bytes=64, bufs=4)
-            hiw = hi[:].bitcast(F32).rearrange("p (g b u) -> p g b u", g=2, u=2)
+            if e % 2 == 0:
+                hi2 = stage.tile([P, 4096], BF16, name="hi", align_bytes=64, bufs=2)
+                his[e // 2] = hi2
+            hi = his[e // 2]
+            hiw = hi[:, 2048 * (e % 2) : 2048 * (e % 2 + 1)].bitcast(F32).rearrange("p (g b u) -> p g b u", g=2, u=2)
             for t in range(2):
                 dst = hiw[:, :, t * P : (t + 1) * P, :]
                 src = xts[(e, t)][:].rearrange("p (g u) b -> p g b u", u=2)
@@ -173,14 +175,14 @@ def tile_softmoedynamics_pb_kernel(tc, h2, logits, W3_bytes, W3_scale, b3, out):
                     nc.vector.tensor_copy(out=dst, in_=src)
                 else:
                     nc.scalar.copy(out=dst, in_=src)
-            his[e] = hi
 
-        def quant_h(e):
-            hc_e = const.tile([P, 512], U32, name="hc%d" % e, align_bytes=64)
-            hs_e = const.tile([P, 512], U8, name="hs%d" % e, align_bytes=64)
-            nc.vector.quantize_mx(out=hc_e[:].bitcast(FP8X4), scales=hs_e[:], in_=his[e][:])
-            hc.append(hc_e)
-            hs.append(hs_e)
+        def quant_h(ep):
+            hc_p = const.tile([P, 1024], U32, name="hc%d" % ep, align_bytes=64)
+            hs_p = const.tile([P, 1024], U8, name="hs%d" % ep, align_bytes=64)
+            nc.vector.quantize_mx(out=hc_p[:].bitcast(FP8X4), scales=hs_p[:], in_=his[ep][:])
+            for ei in range(2):
+                hc.append(hc_p[:, 512 * ei : 512 * (ei + 1)])
+                hs.append(hs_p[:, 512 * ei : 512 * (ei + 1)])
 
         def widen(wbytes, v_slots=()):
             wf = stage.tile([P, 2, 4, 512], BF16, name="wf", bufs=3)
@@ -196,7 +198,7 @@ def tile_softmoedynamics_pb_kernel(tc, h2, logits, W3_bytes, W3_scale, b3, out):
             return wf
 
         def pack(wf, half, key, on_scalar):
-            wi = stage.tile([P, 2048], BF16, name="wi", align_bytes=64)
+            wi = stage.tile([P, 2048], BF16, name="wi", align_bytes=64, bufs=2)
             dst = wi[:].rearrange("p (g c i t) -> p g c t i", g=2, i=8, t=4)
             src = wf[:, :, :, 256 * half : 256 * (half + 1)].rearrange("p g t (c i) -> p g c t i", i=8)
             if on_scalar:
@@ -204,6 +206,21 @@ def tile_softmoedynamics_pb_kernel(tc, h2, logits, W3_bytes, W3_scale, b3, out):
             else:
                 nc.vector.tensor_copy(out=dst, in_=src)
             return wi
+
+        def pack_pair(wf):
+            wi = stage.tile([P, 4096], BF16, name="wi", align_bytes=64, bufs=2)
+            nc.vector.tensor_copy(
+                out=wi[:].rearrange("p (g c i t) -> p g c t i", g=2, i=8, t=4),
+                in_=wf[:].rearrange("p g t (c i) -> p g c t i", i=8),
+            )
+            return wi
+
+        def quant_pair(wi, ep):
+            wc_t = const.tile([P, 1024], U32, name="wc1_%d" % ep, align_bytes=64)
+            ws_t = const.tile([P, 1024], U8, name="ws1_%d" % ep, align_bytes=64)
+            nc.vector.quantize_mx(out=wc_t[:].bitcast(FP8X4), scales=ws_t[:], in_=wi[:])
+            wc[(1, ep)] = wc_t
+            ws[(1, ep)] = ws_t
 
         def quant(wi, key):
             wc_t = const.tile([P, 512], U32, name="wc%d_%d" % key, align_bytes=64)
@@ -229,12 +246,13 @@ def tile_softmoedynamics_pb_kernel(tc, h2, logits, W3_bytes, W3_scale, b3, out):
                 nb = 256 if c == 1 else P
                 dst = zp[:, 0:256] if c == 1 else zp[:, 256:384]
                 for g in range(2):
-                    wcols = slice(g * 256 + (c - 1) * P, g * 256 + c * P)
+                    w0 = g * 512 + (e % 2) * 256 + (c - 1) * P
+                    wcols = slice(w0, w0 + P)
                     hcols = slice(g * 256, g * 256 + nb)
                     nc.tensor.matmul_mx(
                         out=dst,
-                        lhsT=wc[(1, e)][:, wcols].bitcast(FP8X4),
-                        lhsT_scale=ws[(1, e)][:, wcols],
+                        lhsT=wc[(1, e // 2)][:, wcols].bitcast(FP8X4),
+                        lhsT_scale=ws[(1, e // 2)][:, wcols],
                         rhs=hc[e][:, hcols].bitcast(FP8X4),
                         rhs_scale=hs[e][:, hcols],
                         start=(g == 0),
@@ -265,7 +283,7 @@ def tile_softmoedynamics_pb_kernel(tc, h2, logits, W3_bytes, W3_scale, b3, out):
                 evac(0, e, zp[:, ei, :])
 
         def pack_quant_by_pass(wf, half, key):
-            wi = stage.tile([P, 2048], BF16, name="wi", align_bytes=64)
+            wi = stage.tile([P, 2048], BF16, name="wi", align_bytes=64, bufs=2)
             wc_t = const.tile([P, 512], U32, name="wc%d_%d" % key, align_bytes=64)
             ws_t = const.tile([P, 512], U8, name="ws%d_%d" % key, align_bytes=64)
             for g in range(2):
@@ -282,7 +300,7 @@ def tile_softmoedynamics_pb_kernel(tc, h2, logits, W3_bytes, W3_scale, b3, out):
             ws[key] = ws_t
 
         def last_pair_by_pass(wf, half, ep):
-            wi = stage.tile([P, 2048], BF16, name="wi", align_bytes=64)
+            wi = stage.tile([P, 2048], BF16, name="wi", align_bytes=64, bufs=2)
             wc_t = const.tile([P, 512], U32, name="wc0_%d" % ep, align_bytes=64)
             ws_t = const.tile([P, 512], U8, name="ws0_%d" % ep, align_bytes=64)
             zpe = []
@@ -323,14 +341,14 @@ def tile_softmoedynamics_pb_kernel(tc, h2, logits, W3_bytes, W3_scale, b3, out):
             for ei in range(2):
                 e = 2 * ep + ei
                 for g in range(2):
-                    wcols = slice(g * 256, (g + 1) * 256)
+                    wcols = slice(g * 512 + ei * 256, g * 512 + (ei + 1) * 256)
                     hcols = slice(g * 256 + P, g * 256 + 2 * P)
                     nc.tensor.matmul_mx(
                         out=zr[:, ei, :],
                         lhsT=hc[e][:, hcols].bitcast(FP8X4),
                         lhsT_scale=hs[e][:, hcols],
-                        rhs=wc[(1, e)][:, wcols].bitcast(FP8X4),
-                        rhs_scale=ws[(1, e)][:, wcols],
+                        rhs=wc[(1, ep)][:, wcols].bitcast(FP8X4),
+                        rhs_scale=ws[(1, ep)][:, wcols],
                         start=(g == 0),
                         stop=(g == 1),
                     )
@@ -460,12 +478,9 @@ def tile_softmoedynamics_pb_kernel(tc, h2, logits, W3_bytes, W3_scale, b3, out):
             if ep > 0:
                 evac_main1(2 * ep - 2)
                 evac_main1(2 * ep - 1)
-            wia = pack(wfq[ep], 0, (1, 2 * ep), 2 * ep in S_PACK1)
-            wib = pack(wfq[ep], 1, (1, 2 * ep + 1), 2 * ep + 1 in S_PACK1)
-            quant(wia, (1, 2 * ep))
-            quant(wib, (1, 2 * ep + 1))
-            quant_h(2 * ep)
-            quant_h(2 * ep + 1)
+            wip = pack_pair(wfq[ep])
+            quant_h(ep)
+            quant_pair(wip, ep)
             if ep < 3:
                 empty_h(2 * ep + 2)
                 empty_h(2 * ep + 3)

@@ -330,8 +330,15 @@ def tile_softmoedynamics_pb_kernel(tc, h2, logits, W3_bytes, W3_scale, b3, out):
                         start=(g == 0),
                         stop=(g == 1),
                     )
-            for ei in range(2):
-                evac(0, 2 * ep + ei, zpe[ei][:])
+            for hb in range(2):
+                for ei in range(2):
+                    nc.scalar.activation(
+                        out=zs[0][:, 8 * hb : 8 * hb + 8, 2 * ep + ei, :],
+                        in_=zpe[ei][:, P * hb : P * (hb + 1)].rearrange("p (j b) -> p j b", b=16),
+                        func=ACT.Identity,
+                        bias=b3T[:, 3 * (2 * ep + ei) : 3 * (2 * ep + ei) + 1],
+                        scale=1.0,
+                    )
 
         zrs = {}
 

@@ -405,7 +405,9 @@ def tile_softmoedynamics_pb_kernel(tc, h2, logits, W3_bytes, W3_scale, b3, out):
                 nc.vector.scalar_tensor_tensor(
                     out=obs[:, n, :], in0=zb[:, e, :], scalar=cs, in1=obs[:, n, :], op0=ALU.mult, op1=ALU.add
                 )
-            if e == E - 1 and n % 2 == 1:
+            if e == E - 1 and n >= NA - 2:
+                nc.sync.dma_start(out=outv[:, 1, n, NT1:L], in_=obs[:, n, :])
+            elif e == E - 1 and n % 2 == 1:
                 nc.sync.dma_start(out=outv[:, 1, n - 1 : n + 1, NT1:L], in_=obs[:, n - 1 : n + 1, :])
 
         held = {}

@@ -406,9 +406,9 @@ def tile_softmoedynamics_pb_kernel(tc, h2, logits, W3_bytes, W3_scale, b3, out):
                     out=obs[:, n, :], in0=zb[:, e, :], scalar=cs, in1=obs[:, n, :], op0=ALU.mult, op1=ALU.add
                 )
             if e == E - 1 and n >= NA - 2:
-                nc.sync.dma_start(out=outv[:, 1, n, NT1:L], in_=obs[:, n, :])
+                nc.scalar.dma_start(out=outv[:, 1, n, NT1:L], in_=obs[:, n, :])
             elif e == E - 1 and n % 2 == 1:
-                nc.sync.dma_start(out=outv[:, 1, n - 1 : n + 1, NT1:L], in_=obs[:, n - 1 : n + 1, :])
+                nc.scalar.dma_start(out=outv[:, 1, n - 1 : n + 1, NT1:L], in_=obs[:, n - 1 : n + 1, :])
 
         held = {}
 

from contextlib import ExitStack

import concourse.mybir as mybir
from concourse.masks import make_identity

F32 = mybir.dt.float32
BF16 = mybir.dt.bfloat16
U32 = mybir.dt.uint32
U8 = mybir.dt.uint8
FP8 = mybir.dt.float8_e4m3fn
FP8X4 = mybir.dt.float8_e4m3fn_x4
ALU = mybir.AluOpType
ACT = mybir.ActivationFunctionType
AX = mybir.AxisListType

B, NA, E, K, L = 256, 8, 8, 1024, 384
P = 128
NR = 160
NT1 = L - NR
FLOPS = 2 * B * E * K * L + 2 * B * NA * E * L

S_PACK0 = (0, 1, 2, 3)
UNITS = (
    (2, 0, 4), (2, 4, 4), (1, 0, 4), (1, 4, 4), (1, 8, 4), (1, 12, 4), (0, 0, 4), (0, 4, 4), (0, 8, 4), (0, 12, 2), (0, 14, 2)
)
G_MULT = UNITS[0:8]
V_H2 = (0,)


def tile_softmoedynamics_pb_kernel(tc, h2, logits, W3_bytes, W3_scale, b3, out):
    nc = tc.nc
    with ExitStack() as ctx:
        const = ctx.enter_context(tc.tile_pool(name="const", bufs=1))
        loads = ctx.enter_context(tc.tile_pool(name="loads", bufs=4))
        stage = ctx.enter_context(tc.tile_pool(name="stage", bufs=3))
        work = ctx.enter_context(tc.tile_pool(name="work", bufs=5))
        psA = ctx.enter_context(tc.psum_pool(name="psA", bufs=4))
        psB = ctx.enter_context(tc.psum_pool(name="psB", bufs=2))
        psC = ctx.enter_context(tc.psum_pool(name="psC", bufs=2))

        lg = const.tile([P, 2, NA * E], BF16, name="lg")
        nc.sync.dma_start(out=lg[:], in_=logits.rearrange("(t p) n e -> p t (n e)", p=P))
        sc = const.tile([P, 2, 4], F32, name="sc")
        nc.sync.dma_start(
            out=sc[:],
            in_=W3_scale.rearrange("o k u -> (o k u)").rearrange("(g p t) -> p g t", p=P, t=4),
        )
        h2v = h2.rearrange("(t p) e k -> p t e k", p=P)
        wb1, wb0, hraw = [], [], []

        def load_h(e):
            hraw_e = loads.tile([P, 2, K], BF16, name="hraw")
            nc.sync.dma_start(out=hraw_e[:], in_=h2v[:, :, e, :])
            hraw.append(hraw_e)

        def load_w1(ep):
            wb1_t = const.tile([P, 2, 4, 2, 256], U8, name="wbytes1_%d" % ep)
            wb1.append(wb1_t)
            for g in range(2):
                for ei in range(2):
                    nc.sync.dma_start(
                        out=wb1_t[:, g, :, ei, :],
                        in_=W3_bytes[2 * ep + ei, g * 512 : (g + 1) * 512, P:L].rearrange("(p t) n -> p t n", t=4),
                    )

        b3pad = const.tile([P, P], BF16, name="b3pad")
        nc.gpsimd.memset(b3pad[:], 0.0)
        load_w1(0)
        load_h(0)
        load_w1(1)
        load_h(1)
        nc.sync.dma_start(out=b3pad[0 : 3 * E, :], in_=b3.rearrange("e (c p) -> (e c) p", p=P))
        load_h(2)
        load_h(3)
        load_w1(2)
        b3r = const.tile([P, E, NR], BF16, name="b3r")

        def load_b3r(q):
            nc.sync.dma_start(out=b3r[:, 2 * q : 2 * q + 2, :], in_=b3[2 * q : 2 * q + 2, NT1:L].partition_broadcast(P))

        def load_w0(eq):
            wb0_t = const.tile([P, 2, 4, 4, P], U8, name="wbytes0_%d" % eq)
            wb0.append(wb0_t)
            for g in range(2):
                for ei in range(4):
                    nc.sync.dma_start(
                        out=wb0_t[:, g, :, ei, :],
                        in_=W3_bytes[4 * eq + ei, g * 512 : (g + 1) * 512, 0:P].rearrange("(p t) n -> p t n", t=4),
                    )

        load_b3r(0)
        load_h(4)
        load_h(5)
        load_w1(3)
        load_h(6)
        load_h(7)
        load_b3r(1)
        load_w0(0)
        load_b3r(2)
        load_w0(1)
        load_b3r(3)

        warm = const.tile([P, 2], F32, name="warm")
        nc.vector.memset(warm[:], 0.0)
        nc.scalar.activation(out=warm[:, 1:2], in_=warm[:, 0:1], func=ACT.Exp)
        ident_f = const.tile([P, P], F32, name="ident_f")
        make_identity(nc, ident_f[:])
        ident_b = const.tile([P, P], BF16, name="ident_b")
        make_identity(nc, ident_b[:])
        b3ps = psC.tile([P, P], BF16, tag="c", name="b3ps")
        nc.tensor.transpose(b3ps[:], b3pad[:], ident_b[:])
        b3T = const.tile([P, 3 * E], F32, name="b3T")
        nc.vector.tensor_copy(out=b3T[:], in_=b3ps[:, 0 : 3 * E])

        lg3 = lg[:].rearrange("p t (n e) -> p (t n) e", e=E)
        lmx = const.tile([P, 16], F32, name="lmx")
        nc.vector.tensor_reduce(out=lmx[:], in_=lg3, axis=AX.X, op=ALU.max)
        le = const.tile([P, 16, E], F32, name="le")
        nc.vector.tensor_tensor(
            out=le[:], in0=lg3, in1=lmx[:].unsqueeze(2).to_broadcast([P, 16, E]), op=ALU.subtract
        )
        nc.scalar.activation(out=le[:], in_=le[:], func=ACT.Exp)
        lsm = const.tile([P, 16], F32, name="lsm")
        nc.vector.tensor_reduce(out=lsm[:], in_=le[:], axis=AX.X, op=ALU.add)
        lrc = const.tile([P, 16], F32, name="lrc")
        nc.vector.reciprocal(out=lrc[:], in_=lsm[:])
        comb = const.tile([P, 2, E, NA], F32, name="comb")
        nc.vector.tensor_tensor(
            out=comb[:].rearrange("p t e n -> p t n e"),
            in0=le[:].rearrange("p (t n) e -> p t n e", t=2),
            in1=lrc[:].rearrange("p (t n) -> p t n", t=2).unsqueeze(3).to_broadcast([P, 2, NA, E]),
            op=ALU.mult,
        )

        bd = const.tile([P, 16, 16, NA], F32, name="bd")
        nc.gpsimd.memset(bd[:], 0.0)
        park = out.rearrange("b n l -> (b n l)")[0 : B * E * NA]
        nc.sync.dma_start(out=park.rearrange("(t p x) -> p t x", p=P, x=E * NA), in_=comb[:].rearrange("p t e n -> p t (e n)"))
        back = park.rearrange("(j b e n) -> b e j n", b=16, e=E, n=NA)
        for bl in range(16):
            nc.sync.dma_start(out=bd[bl : P : 16, :, bl, :], in_=back[bl])

        zs = []
        for c in range(3):
            zs_c = const.tile([P, 16 if c < 2 else 8, E, 16], F32, name="zs%d" % c)
            zs.append(zs_c)
        zb = const.tile([P, E, NR], F32, name="zb")
        hc, hs = [], []
        wc, ws = {}, {}

        his = {}

        xts = {}

        def turn_h(e):
            words = hraw[e][:].rearrange("p t k -> p (t k)").bitcast(F32)
            for t in range(2):
                xt = psA.tile([P, 4, P], F32, tag="a", name="xt")
                xts[(e, t)] = xt
                for g in range(2):
                    for u in range(2):
                        base = t * 512 + g * 256
                        nc.tensor.transpose(xt[:, 2 * g + u, :], words[:, base + u : base + 256 : 2], ident_f[:])

        def empty_h(e):
            if e % 2 == 0:
                hi2 = stage.tile([P, 4096], BF16, name="hi", align_bytes=64, bufs=2)
                his[e // 2] = hi2
            hi = his[e // 2]
            hiw = hi[:, 2048 * (e % 2) : 2048 * (e % 2 + 1)].bitcast(F32).rearrange("p (g b u) -> p g b u", g=2, u=2)
            for t in range(2):
                dst = hiw[:, :, t * P : (t + 1) * P, :]
                src = xts[(e, t)][:].rearrange("p (g u) b -> p g b u", u=2)
                if t == 1 and e in V_H2:
                    nc.vector.tensor_copy(out=dst, in_=src)
                else:
                    nc.scalar.copy(out=dst, in_=src)

        def quant_h(ep):
            hc_p = const.tile([P, 1024], U32, name="hc%d" % ep, align_bytes=64)
            hs_p = const.tile([P, 1024], U8, name="hs%d" % ep, align_bytes=64)
            nc.vector.quantize_mx(out=hc_p[:].bitcast(FP8X4), scales=hs_p[:], in_=his[ep][:])
            for ei in range(2):
                hc.append(hc_p[:, 512 * ei : 512 * (ei + 1)])
                hs.append(hs_p[:, 512 * ei : 512 * (ei + 1)])

        def widen(wbytes, v_slots=()):
            wf = stage.tile([P, 2, 4, 512], BF16, name="wf", bufs=3)
            for g in range(2):
                for t in range(4):
                    codes = wbytes[:, g, t, :, :].rearrange("p e n -> p (e n)").bitcast(FP8)
                    if t in v_slots:
                        nc.vector.tensor_scalar(
                            out=wf[:, g, t, :], in0=codes, scalar1=sc[:, g, t : t + 1], scalar2=None, op0=ALU.mult
                        )
                    else:
                        nc.scalar.activation(out=wf[:, g, t, :], in_=codes, func=ACT.Copy, scale=sc[:, g, t : t + 1])
            return wf

        def pack(wf, half, key, on_scalar):
            wi = stage.tile([P, 2048], BF16, name="wi", align_bytes=64, bufs=2)
            dst = wi[:].rearrange("p (g c i t) -> p g c t i", g=2, i=8, t=4)
            src = wf[:, :, :, 256 * half : 256 * (half + 1)].rearrange("p g t (c i) -> p g c t i", i=8)
            if on_scalar:
                nc.scalar.copy(out=dst, in_=src)
            else:
                nc.vector.tensor_copy(out=dst, in_=src)
            return wi

        def pack_pair(wf):
            wi = stage.tile([P, 4096], BF16, name="wi", align_bytes=64, bufs=2)
            nc.vector.tensor_copy(
                out=wi[:].rearrange("p (g c i t) -> p g c t i", g=2, i=8, t=4),
                in_=wf[:].rearrange("p g t (c i) -> p g c t i", i=8),
            )
            return wi

        def quant_pair(wi, ep):
            wc_t = const.tile([P, 1024], U32, name="wc1_%d" % ep, align_bytes=64)
            ws_t = const.tile([P, 1024], U8, name="ws1_%d" % ep, align_bytes=64)
            nc.vector.quantize_mx(out=wc_t[:].bitcast(FP8X4), scales=ws_t[:], in_=wi[:])
            wc[(1, ep)] = wc_t
            ws[(1, ep)] = ws_t

        def quant(wi, key):
            wc_t = const.tile([P, 512], U32, name="wc%d_%d" % key, align_bytes=64)
            ws_t = const.tile([P, 512], U8, name="ws%d_%d" % key, align_bytes=64)
            nc.vector.quantize_mx(out=wc_t[:].bitcast(FP8X4), scales=ws_t[:], in_=wi[:])
            wc[key] = wc_t
            ws[key] = ws_t

        def evac(c, e, src):
            nc.scalar.activation(
                out=zs[c][:, :, e, :],
                in_=src.rearrange("p (j b) -> p j b", b=16),
                func=ACT.Identity,
                bias=b3T[:, 3 * e + c : 3 * e + c + 1],
                scale=1.0,
            )

        zp1s = {}

        def mx_main1(e):
            zp = psB.tile([P, 384], F32, tag="b", name="zp1")
            for c in (1, 2):
                nb = 256 if c == 1 else P
                dst = zp[:, 0:256] if c == 1 else zp[:, 256:384]
                for g in range(2):
                    w0 = g * 512 + (e % 2) * 256 + (c - 1) * P
                    wcols = slice(w0, w0 + P)
                    hcols = slice(g * 256, g * 256 + nb)
                    nc.tensor.matmul_mx(
                        out=dst,
                        lhsT=wc[(1, e // 2)][:, wcols].bitcast(FP8X4),
                        lhsT_scale=ws[(1, e // 2)][:, wcols],
                        rhs=hc[e][:, hcols].bitcast(FP8X4),
                        rhs_scale=hs[e][:, hcols],
                        start=(g == 0),
                        stop=(g == 1),
                    )
            zp1s[e] = zp

        def evac_main1(e):
            evac(1, e, zp1s[e][:, 0:256])
            evac(2, e, zp1s[e][:, 256:384])

        def mx_main0(ep):
            zp = psB.tile([P, 2, 256], F32, tag="b", name="zp0")
            for ei in range(2):
                e = 2 * ep + ei
                for g in range(2):
                    wcols = slice((2 * g + ei) * P, (2 * g + ei + 1) * P)
                    hcols = slice(g * 256, (g + 1) * 256)
                    nc.tensor.matmul_mx(
                        out=zp[:, ei, :],
                        lhsT=wc[(0, ep)][:, wcols].bitcast(FP8X4),
                        lhsT_scale=ws[(0, ep)][:, wcols],
                        rhs=hc[e][:, hcols].bitcast(FP8X4),
                        rhs_scale=hs[e][:, hcols],
                        start=(g == 0),
                        stop=(g == 1),
                    )
                evac(0, e, zp[:, ei, :])

        def pack_quant_by_pass(wf, half, key):
            wi = stage.tile([P, 2048], BF16, name="wi", align_bytes=64, bufs=2)
            wc_t = const.tile([P, 512], U32, name="wc%d_%d" % key, align_bytes=64)
            ws_t = const.tile([P, 512], U8, name="ws%d_%d" % key, align_bytes=64)
            for g in range(2):
                nc.scalar.copy(
                    out=wi[:, g * 1024 : (g + 1) * 1024].rearrange("p (c i t) -> p c t i", i=8, t=4),
                    in_=wf[:, g, :, 256 * half : 256 * (half + 1)].rearrange("p t (c i) -> p c t i", i=8),
                )
                nc.vector.quantize_mx(
                    out=wc_t[:, g * 256 : (g + 1) * 256].bitcast(FP8X4),
                    scales=ws_t[:, g * 256 : (g + 1) * 256],
                    in_=wi[:, g * 1024 : (g + 1) * 1024],
                )
            wc[key] = wc_t
            ws[key] = ws_t

        def last_pair_by_pass(wf, half, ep):
            wi = stage.tile([P, 2048], BF16, name="wi", align_bytes=64, bufs=2)
            wc_t = const.tile([P, 512], U32, name="wc0_%d" % ep, align_bytes=64)
            ws_t = const.tile([P, 512], U8, name="ws0_%d" % ep, align_bytes=64)
            zpe = []
            for ei in range(2):
                zp = psB.tile([P, 256], F32, tag="b", name="zp0e")
                zpe.append(zp)
            for g in range(2):
                nc.scalar.copy(
                    out=wi[:, g * 1024 : (g + 1) * 1024].rearrange("p (c i t) -> p c t i", i=8, t=4),
                    in_=wf[:, g, :, 256 * half : 256 * (half + 1)].rearrange("p t (c i) -> p c t i", i=8),
                )
                nc.vector.quantize_mx(
                    out=wc_t[:, g * 256 : (g + 1) * 256].bitcast(FP8X4),
                    scales=ws_t[:, g * 256 : (g + 1) * 256],
                    in_=wi[:, g * 1024 : (g + 1) * 1024],
                )
                for ei in range(2):
                    e = 2 * ep + ei
                    wcols = slice((2 * g + ei) * P, (2 * g + ei + 1) * P)
                    hcols = slice(g * 256, (g + 1) * 256)
                    nc.tensor.matmul_mx(
                        out=zpe[ei][:],
                        lhsT=wc_t[:, wcols].bitcast(FP8X4),
                        lhsT_scale=ws_t[:, wcols],
                        rhs=hc[e][:, hcols].bitcast(FP8X4),
                        rhs_scale=hs[e][:, hcols],
                        start=(g == 0),
                        stop=(g == 1),
                    )
            for hb in range(2):
                for ei in range(2):
                    nc.scalar.activation(
                        out=zs[0][:, 8 * hb : 8 * hb + 8, 2 * ep + ei, :],
                        in_=zpe[ei][:, P * hb : P * (hb + 1)].rearrange("p (j b) -> p j b", b=16),
                        func=ACT.Identity,
                        bias=b3T[:, 3 * (2 * ep + ei) : 3 * (2 * ep + ei) + 1],
                        scale=1.0,
                    )

        zrs = {}

        def mx_rest(ep):
            zr = psC.tile([P, 2, 256], F32, tag="c", name="zr")
            zrs[ep] = zr
            for ei in range(2):
                e = 2 * ep + ei
                for g in range(2):
                    wcols = slice(g * 512 + ei * 256, g * 512 + (ei + 1) * 256)
                    hcols = slice(g * 256 + P, g * 256 + 2 * P)
                    nc.tensor.matmul_mx(
                        out=zr[:, ei, :],
                        lhsT=hc[e][:, hcols].bitcast(FP8X4),
                        lhsT_scale=hs[e][:, hcols],
                        rhs=wc[(1, ep)][:, wcols].bitcast(FP8X4),
                        rhs_scale=ws[(1, ep)][:, wcols],
                        start=(g == 0),
                        stop=(g == 1),
                    )

        def rest_add(ep):
            nc.vector.tensor_tensor(
                out=zb[:, 2 * ep : 2 * ep + 2, :],
                in0=zrs[ep][:, :, 256 - NR : 256],
                in1=b3r[:, 2 * ep : 2 * ep + 2, :],
                op=ALU.add,
            )

        NG = 2 * NR // 8

        def zb_groups(q):
            return zb[:, 2 * q : 2 * q + 2, :].rearrange("p e (g i) -> p (e g) i", i=8)

        def rest_simnorm_a(q):
            zbg = zb_groups(q)
            rmx = const.tile([P, NG], F32, name="rmx%d" % q)
            nc.vector.tensor_reduce(out=rmx[:], in_=zbg, axis=AX.X, op=ALU.max)
            nc.vector.tensor_tensor(
                out=zbg, in0=zbg, in1=rmx[:].unsqueeze(2).to_broadcast([P, NG, 8]), op=ALU.subtract
            )
            nc.scalar.activation(out=zbg, in_=zbg, func=ACT.Exp)

        def rest_simnorm_b(q):
            zbg = zb_groups(q)
            rsm = const.tile([P, NG], F32, name="rsm%d" % q)
            nc.vector.tensor_reduce(out=rsm[:], in_=zbg, axis=AX.X, op=ALU.add)
            rrc = const.tile([P, NG], F32, name="rrc%d" % q)
            nc.vector.reciprocal(out=rrc[:], in_=rsm[:])
            nc.vector.tensor_tensor(
                out=zbg, in0=zbg, in1=rrc[:].unsqueeze(2).to_broadcast([P, NG, 8]), op=ALU.mult
            )

        out_flat = out.rearrange("b n l -> (b n) l")
        out_tiles = out_flat.rearrange("(j p) l -> p j l", p=P)
        outv = out.rearrange("(t p) n l -> p t n l", p=P)
        obs = const.tile([P, NA, NR], F32, name="obs")

        def rest_combine(e, n):
            cs = comb[:, 1, e, n : n + 1]
            if e == 0:
                nc.vector.tensor_scalar(out=obs[:, n, :], in0=zb[:, e, :], scalar1=cs, scalar2=None, op0=ALU.mult)
            else:
                nc.vector.scalar_tensor_tensor(
                    out=obs[:, n, :], in0=zb[:, e, :], scalar=cs, in1=obs[:, n, :], op0=ALU.mult, op1=ALU.add
                )
            if e == E - 1 and n >= NA - 2:
                nc.scalar.dma_start(out=outv[:, 1, n, NT1:L], in_=obs[:, n, :])
            elif e == E - 1 and n % 2 == 1:
                nc.scalar.dma_start(out=outv[:, 1, n - 1 : n + 1, NT1:L], in_=obs[:, n - 1 : n + 1, :])

        held = {}

        def width(c, j0):
            return NT1 - P if (c == 1 and j0 >= 8) else P

        def finish_a(c, j0, nt):
            w = width(c, j0)
            ng = w // 8
            ztp = psA.tile([P, 4, P], F32, tag="a", name="ztp")
            for jj in range(nt):
                nc.tensor.transpose(
                    ztp[:, jj, :], zs[c][:, j0 + jj, :, :].rearrange("p e b -> p (e b)"), ident_f[:]
                )
            z4 = ztp[:, 0:nt, 0:w].rearrange("p j (g i) -> p j g i", i=8)
            mx = work.tile([P, nt, ng], F32, name="mx%d" % w)
            nc.vector.tensor_reduce(out=mx[:], in_=z4, axis=AX.X, op=ALU.max)
            ex = work.tile([P, nt, ng, 8], F32, name="ex%d" % w)
            nc.vector.tensor_tensor(
                out=ex[:], in0=z4, in1=mx[:].unsqueeze(3).to_broadcast([P, nt, ng, 8]), op=ALU.subtract
            )
            nc.scalar.activation(out=ex[:], in_=ex[:], func=ACT.Exp)
            held[(c, j0)] = ex

        def finish_b(c, j0, nt):
            w = width(c, j0)
            ng = w // 8
            ex = held[(c, j0)]
            sm = work.tile([P, nt, ng], F32, name="sm%d" % w)
            nc.vector.tensor_reduce(out=sm[:], in_=ex[:], axis=AX.X, op=ALU.add)
            rc = work.tile([P, nt, ng], F32, name="rc%d" % w)
            nc.vector.reciprocal(out=rc[:], in_=sm[:])
            eng = nc.gpsimd if (c, j0, nt) in G_MULT else nc.vector
            eng.tensor_tensor(
                out=ex[:], in0=ex[:], in1=rc[:].unsqueeze(3).to_broadcast([P, nt, ng, 8]), op=ALU.mult
            )

        def finish_c(c, j0, nt):
            w = width(c, j0)
            ex = held[(c, j0)]
            op = psC.tile([P, 4, P], F32, tag="c", name="op")
            for jj in range(nt):
                nc.tensor.matmul(
                    op[:, jj, 0:w],
                    lhsT=bd[:, j0 + jj, :, :].rearrange("p b n -> p (b n)"),
                    rhs=ex[:, jj, :, :].rearrange("p g i -> p (g i)"),
                    start=True,
                    stop=True,
                )
            ot = work.tile([P, nt, w], F32, name="ot%d" % w)
            nc.scalar.copy(out=ot[:], in_=op[:, 0:nt, 0:w])
            nc.sync.dma_start(out=out_tiles[:, j0 : j0 + nt, c * P : c * P + w], in_=ot[:])

        rest = [(e, n) for e in range(E - 3) for n in range(NA)]
        rest.extend([(e, n2 + i) for n2 in range(0, NA, 2) for e in range(E - 3, E) for i in range(2)])
        done = [0]

        def rest_units(k):
            for en in rest[done[0] : done[0] + k]:
                rest_combine(en[0], en[1])
            done[0] = done[0] + k

        wfq = []
        wfq.append(widen(wb1[0], (2, 3)))
        turn_h(0)
        empty_h(0)
        turn_h(1)
        empty_h(1)
        for ep in range(4):
            if ep < 3:
                turn_h(2 * ep + 2)
                turn_h(2 * ep + 3)
                wfq.append(widen(wb1[ep + 1], (3,) if ep < 2 else ()))
            else:
                wfq.append(widen(wb0[0]))
            if ep > 0:
                evac_main1(2 * ep - 2)
                evac_main1(2 * ep - 1)
            wip = pack_pair(wfq[ep])
            quant_h(ep)
            quant_pair(wip, ep)
            if ep < 3:
                empty_h(2 * ep + 2)
                empty_h(2 * ep + 3)
            mx_main1(2 * ep)
            mx_main1(2 * ep + 1)
            mx_rest(ep)
            if ep > 0:
                rest_add(ep - 1)
                rest_simnorm_a(ep - 1)
            if ep > 1:
                rest_simnorm_b(ep - 2)
                rest_units(8 if ep == 2 else 24)
        evac_main1(6)
        evac_main1(7)
        rest_add(3)
        rest_simnorm_a(3)
        rest_simnorm_b(2)
        fill = [4, 4, 0, 0, 0, 0, 0, 0, 0, 0, 0]
        for i in range(len(UNITS)):
            if i < 4:
                if i == 1:
                    wfq.append(widen(wb0[1], (2, 3)))
                if i < 2:
                    quant(pack(wfq[4 + i // 2], i % 2, (0, i), i in S_PACK0), (0, i))
                    mx_main0(i)
                elif i == 2:
                    pack_quant_by_pass(wfq[4 + i // 2], i % 2, (0, i))
                    mx_main0(i)
                else:
                    last_pair_by_pass(wfq[4 + i // 2], i % 2, i)
            finish_a(UNITS[i][0], UNITS[i][1], UNITS[i][2])
            if i == 1:
                rest_simnorm_b(3)
            rest_units(fill[i])
            if i > 0:
                finish_b(UNITS[i - 1][0], UNITS[i - 1][1], UNITS[i - 1][2])
            if i > 1:
                finish_c(UNITS[i - 2][0], UNITS[i - 2][1], UNITS[i - 2][2])
        finish_c(UNITS[-2][0], UNITS[-2][1], UNITS[-2][2])
        finish_b(UNITS[-1][0], UNITS[-1][1], UNITS[-1][2])
        finish_c(UNITS[-1][0], UNITS[-1][1], UNITS[-1][2])
        rest_units(len(rest) - done[0])
